import numpy as np
import ml_dtypes


def mxq(x, axis, fmt="e4m3"):
    dtype, down = {"e4m3": (ml_dtypes.float8_e4m3fn, 7), "e5m2": (ml_dtypes.float8_e5m2, 14)}[fmt]
    v = np.moveaxis(np.asarray(x, np.float32).astype(ml_dtypes.bfloat16).astype(np.float64), axis, -1)
    blocks = v.reshape(v.shape[:-1] + (-1, 32))
    amax = np.abs(blocks).max(-1, keepdims=True)
    byte = np.maximum(np.where(amax > 0, np.frexp(amax)[1] - 1 + 127, 0) - down, 1)
    scale = np.exp2(byte - 127.0)
    codes = (blocks / scale).astype(np.float32).astype(dtype).astype(np.float64)
    return np.moveaxis((codes * scale).reshape(v.shape), -1, axis)


WIDE = False


def mx_kscale(k):
    if not WIDE:
        return np.ones(k)
    levels = np.array([10, -10, 5, -5, 0])
    if k % 512:
        return np.exp2(np.random.permutation(np.resize(levels, k // 32))).repeat(32)
    a = np.empty((k // 512, 16))
    for p in range(k // 512):
        a[p, :8] = np.random.permutation(np.resize(levels, 8))
        for g in range(8):
            far = levels[np.abs(levels - a[p, g]) >= 10]
            a[p, g + 8] = far[np.random.randint(len(far))]
    return np.exp2(a.ravel()).repeat(32)


BF16 = ml_dtypes.bfloat16


def bf(x):
    return np.asarray(x, np.float32).astype(BF16)


def f64(x):
    return np.asarray(x).astype(np.float64)


B, P, WS, D, H = 2, 64, 8, 512, 8
WN = P // WS
N = WS * WS
SHIFT = WS // 2
LN_EPS = 1e-5


def layer_norm(x, g, b):
    mu = x.mean(-1, keepdims=True)
    var = x.var(-1, keepdims=True)
    return (x - mu) / np.sqrt(var + LN_EPS) * g + b


def window_merge(win):
    x = win.reshape(B, WN, WN, WS, WS, D).transpose(0, 1, 3, 2, 4, 5)
    return x.reshape(B, P, P, D)


def setup_inputs():
    s, t = mx_kscale(D), mx_kscale(D)
    x_mid = np.random.standard_normal((B, P * P, D)) * 1.4 + np.random.standard_normal((B, P * P, 1)) * 0.5
    return {"attn_win": bf(np.random.standard_normal((B * WN * WN, N, D)) * 0.4 * s),
            "x_mid": bf(x_mid),
            "Wo2": bf(np.random.standard_normal((D, D)) / np.sqrt(D) / s[:, None]),
            "bo2": bf(0.1 * np.random.standard_normal(D)),
            "g4": bf((1.0 + 0.1 * np.random.standard_normal(D)) * t),
            "b4": bf(0.1 * np.random.standard_normal(D) * t),
            "Wl": bf(np.random.standard_normal((D, D)) / np.sqrt(D) / t[:, None]),
            "bl": bf(0.1 * np.random.standard_normal(D))}


def reference(attn_win, x_mid, Wo2, bo2, g4, b4, Wl, bl):
    a = (mxq(f64(attn_win), 2, "e4m3") @ mxq(f64(Wo2), 0, "e4m3")) + f64(bo2)
    a = np.roll(window_merge(a), (-SHIFT, -SHIFT), axis=(1, 2)).reshape(B, P * P, D)
    x = f64(x_mid) + a
    h = layer_norm(x, f64(g4), f64(b4))
    return x + (mxq(h, 2, "e4m3") @ mxq(f64(Wl), 0, "e4m3")) + f64(bl)

@@ -1,0 +1,329 @@
+from contextlib import ExitStack
+
+import concourse.mybir as mybir
+from concourse.masks import make_identity
+
+F32 = mybir.dt.float32
+BF16 = mybir.dt.bfloat16
+U32 = mybir.dt.uint32
+U8 = mybir.dt.uint8
+FP8X4 = mybir.dt.float8_e4m3fn_x4
+ADD = mybir.AluOpType.add
+MULT = mybir.AluOpType.mult
+ACT = mybir.ActivationFunctionType
+
+P = 128
+D = 512
+PACK = 4
+QUAD = 4
+GROUP = P * QUAD
+IMAGES = 2
+WINDOW_ROWS = 8
+WS = 8
+GROUPS = IMAGES * WINDOW_ROWS
+IMAGE_TOKENS = WINDOW_ROWS * GROUP
+ROW_QUADS = 16
+SHIFT_TOKENS = GROUP // 2
+LN_EPS = 1e-5
+Z_BANKS = 3
+
+FLOPS = 2 * 2 * IMAGES * IMAGE_TOKENS * D * D
+
+
+def quads(flat, first, count):
+    return flat[first : first + count, :].rearrange("(p q) d -> p q d", q=QUAD)
+
+
+def image_pieces(g):
+    image, window_row = divmod(g, WINDOW_ROWS)
+    base = image * IMAGE_TOKENS
+    if window_row == 0:
+        half = P // 2
+        return [(0, half, base + IMAGE_TOKENS - SHIFT_TOKENS), (half, half, base)]
+    return [(0, P, base + window_row * GROUP - SHIFT_TOKENS)]
+
+
+def quantise_weight(nc, stage, keep, raw, label):
+    grouped = stage.tile([P, D, PACK], BF16, name="grouped_" + label, align_bytes=64)
+    nc.vector.tensor_copy(out=grouped[:], in_=raw[:].rearrange("p t n -> p n t"))
+    codes = keep.tile([P, D], U32, name="codes_" + label, align_bytes=64)
+    scales = keep.tile([P, D], U8, name="scales_" + label, align_bytes=64)
+    nc.vector.quantize_mx(
+        out=codes[:].bitcast(FP8X4), scales=scales[:], in_=grouped[:].rearrange("p n t -> p (n t)")
+    )
+    return codes, scales
+
+
+def tile_successiveswintransfomerblock_pb_t_kernel(tc, attn_win, x_mid, Wo2, bo2, g4, b4, Wl, bl, out):
+    nc = tc.nc
+    attn_flat = attn_win.flatten_outer_dims()
+    x_flat = x_mid.flatten_outer_dims()
+    out_flat = out.flatten_outer_dims()
+
+    with ExitStack() as ctx:
+        keep = ctx.enter_context(tc.tile_pool(name="keep", bufs=1))
+        stage = ctx.enter_context(tc.tile_pool(name="stage", bufs=1))
+        loads = ctx.enter_context(tc.tile_pool(name="loads", bufs=3))
+        work = ctx.enter_context(tc.tile_pool(name="work", bufs=2))
+        resid = ctx.enter_context(tc.tile_pool(name="resid", bufs=6))
+        stats = ctx.enter_context(tc.tile_pool(name="stats", bufs=4))
+        psum_at = ctx.enter_context(tc.psum_pool(name="psum_at", bufs=2))
+        psum_mm = ctx.enter_context(tc.psum_pool(name="psum_mm", bufs=3))
+        psum_zt = ctx.enter_context(tc.psum_pool(name="psum_zt", bufs=Z_BANKS))
+        ctx.enter_context(tc.manual_schedule())
+
+        eps_col = keep.tile([P, 1], F32, name="eps_col")
+        nc.vector.memset(eps_col[:], LN_EPS)
+
+        wo_raw = stage.tile([P, PACK, D], BF16, name="wo_raw")
+        nc.sync.dma_start(out=wo_raw[:], in_=Wo2.rearrange("(p t) n -> p t n", t=PACK))
+        wl_raw = stage.tile([P, PACK, D], BF16, name="wl_raw")
+        nc.sync.dma_start(out=wl_raw[:], in_=Wl.rearrange("(p t) n -> p t n", t=PACK))
+        g_raw = keep.tile([P, PACK], BF16, name="g_raw")
+        nc.scalar.dma_start(out=g_raw[:], in_=g4.rearrange("(p t) -> p t", t=PACK))
+        b_raw = keep.tile([P, PACK], BF16, name="b_raw")
+        nc.scalar.dma_start(out=b_raw[:], in_=b4.rearrange("(p t) -> p t", t=PACK))
+        bo2_all = keep.tile([P, D], BF16, name="bo2_all")
+        nc.scalar.dma_start(out=bo2_all[:], in_=bo2.partition_broadcast(P))
+        bl_all = keep.tile([P, D], BF16, name="bl_all")
+        nc.scalar.dma_start(out=bl_all[:], in_=bl.partition_broadcast(P))
+
+        ident = keep.tile([P, P], F32, name="ident")
+        make_identity(nc, ident[:])
+        by_row = keep.tile([P, P], F32, name="by_row")
+        nc.vector.tensor_copy(
+            out=by_row[:].rearrange("p (r w h) -> p r w h", r=WS, w=WS),
+            in_=ident[:].rearrange("p (w r h) -> p r w h", w=WS, r=WS),
+        )
+        to_image = keep.tile([P, P], F32, name="to_image")
+        unrolled = by_row[:].rearrange("p (r m) -> p r m", m=ROW_QUADS)
+        rolled = to_image[:].rearrange("p (r m) -> p r m", m=ROW_QUADS)
+        nc.vector.tensor_copy(out=rolled[:, :, 0 : ROW_QUADS - 1], in_=unrolled[:, :, 1:ROW_QUADS])
+        nc.vector.tensor_copy(out=rolled[:, :, ROW_QUADS - 1 : ROW_QUADS], in_=unrolled[:, :, 0:1])
+
+        wo_codes, wo_scales = quantise_weight(nc, stage, keep, wo_raw, "wo")
+        wl_codes, wl_scales = quantise_weight(nc, stage, keep, wl_raw, "wl")
+
+        g_col = keep.tile([P, PACK], F32, name="g_col")
+        nc.vector.tensor_copy(out=g_col[:], in_=g_raw[:])
+        b_col = keep.tile([P, PACK], F32, name="b_col")
+        nc.vector.tensor_copy(out=b_col[:], in_=b_raw[:])
+
+        live = {}
+
+        def load(g):
+            if not 0 <= g < GROUPS:
+                return
+            attn_sb = loads.tile([P, QUAD, D], BF16, name="attn_sb")
+            nc.sync.dma_start(out=attn_sb[:], in_=quads(attn_flat, g * GROUP, GROUP))
+            xm_sb = loads.tile([P, QUAD, D], BF16, name="xm_sb")
+            for first_p, n_p, first_token in image_pieces(g):
+                nc.sync.dma_start(out=xm_sb[first_p : first_p + n_p], in_=quads(x_flat, first_token, n_p * QUAD))
+            live["attn_sb", g] = attn_sb
+            live["xm_sb", g] = xm_sb
+
+        def attn_transpose(g):
+            if not 0 <= g < GROUPS:
+                return
+            attn_words = live["attn_sb", g][:].bitcast(F32)
+            for pair in range(QUAD // 2):
+                a_t = psum_at.tile([P, 2, 2, P], F32, name="a_t")
+                for s in range(2):
+                    for u in range(2):
+                        nc.tensor.transpose(
+                            a_t[:, s, u, :], attn_words[:, 2 * pair + s, u : 2 * P : 2], to_image[:]
+                        )
+                live["a_t", g, pair] = a_t
+
+        def attn_copy_out(g):
+            if not 0 <= g < GROUPS:
+                return
+            a_grouped = work.tile([P, QUAD, P, PACK], BF16, name="a_grouped", bufs=3, align_bytes=64)
+            for pair in range(QUAD // 2):
+                nc.scalar.copy(
+                    out=a_grouped[:, 2 * pair : 2 * pair + 2].bitcast(F32),
+                    in_=live["a_t", g, pair][:].rearrange("p s u r -> p s r u"),
+                )
+            live["a_grouped", g] = a_grouped
+
+        def quantise_attn(g):
+            if not 0 <= g < GROUPS:
+                return
+            a_codes = work.tile([P, GROUP], U32, name="a_codes", align_bytes=64)
+            a_scales = work.tile([P, GROUP], U8, name="a_scales", align_bytes=64)
+            nc.vector.quantize_mx(
+                out=a_codes[:].bitcast(FP8X4),
+                scales=a_scales[:],
+                in_=live["a_grouped", g][:].rearrange("p q r t -> p (q r t)"),
+            )
+            live["a_codes", g] = a_codes
+            live["a_scales", g] = a_scales
+
+        def add_bo2(g):
+            if not 0 <= g < GROUPS:
+                return
+            x = resid.tile([P, QUAD, D], F32, name="x")
+            nc.vector.tensor_tensor(
+                out=x[:], in0=live["xm_sb", g][:], in1=bo2_all[:].unsqueeze(1).to_broadcast([P, QUAD, D]), op=ADD
+            )
+            live["x", g] = x
+
+        def first_product(g):
+            if not 0 <= g < GROUPS:
+                return
+            x = live["x", g]
+            x_sum = stats.tile([P, QUAD], F32, name="x_sum")
+            for q in range(QUAD):
+                tokens = slice(q * P, (q + 1) * P)
+                acc1 = psum_mm.tile([P, D], F32, name="acc1", tag="acc")
+                nc.tensor.matmul_mx(
+                    out=acc1[:],
+                    lhsT=live["a_codes", g][:, tokens].bitcast(FP8X4),
+                    lhsT_scale=live["a_scales", g][:, tokens],
+                    rhs=wo_codes[:].bitcast(FP8X4),
+                    rhs_scale=wo_scales[:],
+                    start=True,
+                    stop=True,
+                )
+                nc.vector.scalar_tensor_tensor(
+                    out=x[:, q, :],
+                    in0=acc1[:],
+                    scalar=1.0,
+                    in1=x[:, q, :],
+                    op0=MULT,
+                    op1=ADD,
+                    accum_out=x_sum[:, q : q + 1],
+                )
+            neg_mean = stats.tile([P, QUAD], F32, name="neg_mean")
+            nc.gpsimd.tensor_scalar(out=neg_mean[:], in0=x_sum[:], scalar1=-1.0 / D, scalar2=0.0, op0=MULT, op1=ADD)
+            live["neg_mean", g] = neg_mean
+
+        def variance(g):
+            if not 0 <= g < GROUPS:
+                return
+            neg_mean = live["neg_mean", g]
+            sq_sum = stats.tile([P, QUAD], F32, name="sq_sum")
+            for q in range(QUAD):
+                squares = work.tile([P, D], BF16, name="squares")
+                nc.scalar.activation(
+                    out=squares[:],
+                    in_=live["x", g][:, q, :],
+                    func=ACT.Square,
+                    bias=neg_mean[:, q : q + 1],
+                    scale=1.0,
+                    accum_out=sq_sum[:, q : q + 1],
+                )
+            rstd = stats.tile([P, QUAD], F32, name="rstd")
+            nc.scalar.activation(
+                out=rstd[:], in_=sq_sum[:], func=ACT.Abs_reciprocal_sqrt, bias=eps_col[:], scale=1.0 / D
+            )
+            shift = stats.tile([P, QUAD], F32, name="shift")
+            nc.gpsimd.tensor_tensor(out=shift[:], in0=neg_mean[:], in1=rstd[:], op=MULT)
+            live["rstd", g] = rstd
+            live["shift", g] = shift
+
+        def normalise(g):
+            if not 0 <= g < GROUPS:
+                return
+            z = work.tile([P, QUAD, D], F32, name="z")
+            for q in range(QUAD):
+                nc.scalar.activation(
+                    out=z[:, q, :].rearrange("p (t m) -> p t m", t=PACK),
+                    in_=live["x", g][:, q, :].rearrange("p (m t) -> p t m", t=PACK),
+                    func=ACT.Identity,
+                    bias=live["shift", g][:, q : q + 1],
+                    scale=live["rstd", g][:, q : q + 1],
+                )
+            live["z", g] = z
+
+        def z_transpose(g, t):
+            if not 0 <= g < GROUPS:
+                return
+            z_t = psum_zt.tile([P, GROUP], F32, name="z_t")
+            for q in range(QUAD):
+                nc.tensor.transpose(z_t[:, q * P : (q + 1) * P], live["z", g][:, q, t * P : (t + 1) * P], ident[:])
+            live["z_t", g, t] = z_t
+
+        def gain_and_bias(g, t):
+            if not 0 <= g < GROUPS:
+                return
+            if t == 0:
+                live["h_t", g] = work.tile([P, PACK, GROUP], BF16, name="h_t")
+            nc.scalar.activation(
+                out=live["h_t", g][:, t, :],
+                in_=live["z_t", g, t][:],
+                func=ACT.Identity,
+                bias=b_col[:, t : t + 1],
+                scale=g_col[:, t : t + 1],
+            )
+
+        def regroup_h(g):
+            if not 0 <= g < GROUPS:
+                return
+            h_grouped = work.tile([P, GROUP, PACK], BF16, name="h_grouped", align_bytes=64)
+            nc.scalar.copy(
+                out=h_grouped[:].rearrange("p (c i) t -> p c t i", i=4),
+                in_=live["h_t", g][:].rearrange("p t (c i) -> p c t i", i=4),
+            )
+            live["h_grouped", g] = h_grouped
+
+        def quantise_h(g):
+            if not 0 <= g < GROUPS:
+                return
+            h_codes = work.tile([P, GROUP], U32, name="h_codes", align_bytes=64)
+            h_scales = work.tile([P, GROUP], U8, name="h_scales", align_bytes=64)
+            nc.vector.quantize_mx(
+                out=h_codes[:].bitcast(FP8X4),
+                scales=h_scales[:],
+                in_=live["h_grouped", g][:].rearrange("p r t -> p (r t)"),
+            )
+            live["h_codes", g] = h_codes
+            live["h_scales", g] = h_scales
+
+        def add_bl(g):
+            if not 0 <= g < GROUPS:
+                return
+            x = live["x", g]
+            nc.vector.tensor_tensor(out=x[:], in0=x[:], in1=bl_all[:].unsqueeze(1).to_broadcast([P, QUAD, D]), op=ADD)
+
+        def second_product(g):
+            if not 0 <= g < GROUPS:
+                return
+            x = live["x", g]
+            for q in range(QUAD):
+                tokens = slice(q * P, (q + 1) * P)
+                acc2 = psum_mm.tile([P, D], F32, name="acc2", tag="acc")
+                nc.tensor.matmul_mx(
+                    out=acc2[:],
+                    lhsT=live["h_codes", g][:, tokens].bitcast(FP8X4),
+                    lhsT_scale=live["h_scales", g][:, tokens],
+                    rhs=wl_codes[:].bitcast(FP8X4),
+                    rhs_scale=wl_scales[:],
+                    start=True,
+                    stop=True,
+                )
+                nc.vector.tensor_tensor(out=x[:, q, :], in0=acc2[:], in1=x[:, q, :], op=ADD)
+                for first_p, n_p, first_token in image_pieces(g):
+                    nc.sync.dma_start(
+                        out=quads(out_flat, first_token, n_p * QUAD)[:, q, :], in_=x[first_p : first_p + n_p, q, :]
+                    )
+
+        for step in range(-3, GROUPS + 2):
+            load(step + 3)
+            attn_transpose(step + 2)
+            quantise_h(step - 2)
+            add_bl(step - 1)
+            variance(step)
+            quantise_attn(step + 1)
+            attn_copy_out(step + 2)
+            second_product(step - 2)
+            first_product(step + 1)
+            add_bo2(step + 2)
+            normalise(step)
+            regroup_h(step - 1)
+            for t in range(Z_BANKS):
+                z_transpose(step, t)
+            for t in range(PACK):
+                gain_and_bias(step, t)
+                if t + Z_BANKS < PACK:
+                    z_transpose(step, t + Z_BANKS)

@@ -15,6 +15,7 @@ ACT = mybir.ActivationFunctionType
 P = 128
 D = 512
 PACK = 4
+RUN = 8
 QUAD = 4
 GROUP = P * QUAD
 IMAGES = 2
@@ -72,17 +73,22 @@ def tile_successiveswintransfomerblock_pb_t_kernel(tc, attn_win, x_mid, Wo2, bo2
         psum_zt = ctx.enter_context(tc.psum_pool(name="psum_zt", bufs=Z_BANKS))
         ctx.enter_context(tc.manual_schedule())
 
+        gb_rows = keep.tile([P, P], BF16, name="gb_rows")
+        nc.vector.memset(gb_rows[:], 0.0)
         eps_col = keep.tile([P, 1], F32, name="eps_col")
         nc.vector.memset(eps_col[:], LN_EPS)
 
         wo_raw = stage.tile([P, PACK, D], BF16, name="wo_raw")
         nc.sync.dma_start(out=wo_raw[:], in_=Wo2.rearrange("(p t) n -> p t n", t=PACK))
         wl_raw = stage.tile([P, PACK, D], BF16, name="wl_raw")
-        nc.sync.dma_start(out=wl_raw[:], in_=Wl.rearrange("(p t) n -> p t n", t=PACK))
-        g_raw = keep.tile([P, PACK], BF16, name="g_raw")
-        nc.scalar.dma_start(out=g_raw[:], in_=g4.rearrange("(p t) -> p t", t=PACK))
-        b_raw = keep.tile([P, PACK], BF16, name="b_raw")
-        nc.scalar.dma_start(out=b_raw[:], in_=b4.rearrange("(p t) -> p t", t=PACK))
+        for t in range(PACK):
+            nc.sync.dma_start(out=wl_raw[:, t, :], in_=Wl.rearrange("(b t r) n -> t b r n", t=PACK, r=RUN)[t])
+        for first, vec in ((0, g4), (PACK, b4)):
+            for t in range(PACK):
+                nc.scalar.dma_start(
+                    out=gb_rows[first + t : first + t + 1, :],
+                    in_=vec.rearrange("(o b t r) -> t o b r", o=1, t=PACK, r=RUN)[t],
+                )
         bo2_all = keep.tile([P, D], BF16, name="bo2_all")
         nc.scalar.dma_start(out=bo2_all[:], in_=bo2.partition_broadcast(P))
         bl_all = keep.tile([P, D], BF16, name="bl_all")
@@ -101,13 +107,16 @@ def tile_successiveswintransfomerblock_pb_t_kernel(tc, attn_win, x_mid, Wo2, bo2
         nc.vector.tensor_copy(out=rolled[:, :, 0 : ROW_QUADS - 1], in_=unrolled[:, :, 1:ROW_QUADS])
         nc.vector.tensor_copy(out=rolled[:, :, ROW_QUADS - 1 : ROW_QUADS], in_=unrolled[:, :, 0:1])
 
+        ident_bf = keep.tile([P, P], BF16, name="ident_bf")
+        nc.vector.tensor_copy(out=ident_bf[:], in_=ident[:])
+
         wo_codes, wo_scales = quantise_weight(nc, stage, keep, wo_raw, "wo")
         wl_codes, wl_scales = quantise_weight(nc, stage, keep, wl_raw, "wl")
 
-        g_col = keep.tile([P, PACK], F32, name="g_col")
-        nc.vector.tensor_copy(out=g_col[:], in_=g_raw[:])
-        b_col = keep.tile([P, PACK], F32, name="b_col")
-        nc.vector.tensor_copy(out=b_col[:], in_=b_raw[:])
+        gb_ps = psum_mm.tile([P, P], BF16, name="gb_ps", tag="acc")
+        nc.tensor.transpose(gb_ps[:], gb_rows[:], ident_bf[:])
+        gb_col = keep.tile([P, 2 * PACK], F32, name="gb_col")
+        nc.vector.tensor_copy(out=gb_col[:], in_=gb_ps[:, 0 : 2 * PACK])
 
         live = {}
 
@@ -228,8 +237,8 @@ def tile_successiveswintransfomerblock_pb_t_kernel(tc, attn_win, x_mid, Wo2, bo2
             z = work.tile([P, QUAD, D], F32, name="z")
             for q in range(QUAD):
                 nc.scalar.activation(
-                    out=z[:, q, :].rearrange("p (t m) -> p t m", t=PACK),
-                    in_=live["x", g][:, q, :].rearrange("p (m t) -> p t m", t=PACK),
+                    out=z[:, q, :].rearrange("p (t b r) -> p t b r", t=PACK, r=RUN),
+                    in_=live["x", g][:, q, :].rearrange("p (b t r) -> p t b r", t=PACK, r=RUN),
                     func=ACT.Identity,
                     bias=live["shift", g][:, q : q + 1],
                     scale=live["rstd", g][:, q : q + 1],
@@ -253,8 +262,8 @@ def tile_successiveswintransfomerblock_pb_t_kernel(tc, attn_win, x_mid, Wo2, bo2
                 out=live["h_t", g][:, t, :],
                 in_=live["z_t", g, t][:],
                 func=ACT.Identity,
-                bias=b_col[:, t : t + 1],
-                scale=g_col[:, t : t + 1],
+                bias=gb_col[:, PACK + t : PACK + t + 1],
+                scale=gb_col[:, t : t + 1],
             )
 
         def regroup_h(g):

@@ -18,15 +18,17 @@ PACK = 4
 RUN = 8
 QUAD = 4
 GROUP = P * QUAD
+SLOTS = 2
+UNIT = P * SLOTS
 IMAGES = 2
 WINDOW_ROWS = 8
 WS = 8
 GROUPS = IMAGES * WINDOW_ROWS
+UNITS = GROUPS * QUAD // SLOTS
 IMAGE_TOKENS = WINDOW_ROWS * GROUP
 ROW_QUADS = 16
 SHIFT_TOKENS = GROUP // 2
 LN_EPS = 1e-5
-Z_BANKS = 3
 
 FLOPS = 2 * 2 * IMAGES * IMAGE_TOKENS * D * D
 
@@ -64,35 +66,49 @@ def tile_successiveswintransfomerblock_pb_t_kernel(tc, attn_win, x_mid, Wo2, bo2
     with ExitStack() as ctx:
         keep = ctx.enter_context(tc.tile_pool(name="keep", bufs=1))
         stage = ctx.enter_context(tc.tile_pool(name="stage", bufs=1))
-        loads = ctx.enter_context(tc.tile_pool(name="loads", bufs=3))
-        work = ctx.enter_context(tc.tile_pool(name="work", bufs=2))
-        resid = ctx.enter_context(tc.tile_pool(name="resid", bufs=6))
+        loads = ctx.enter_context(tc.tile_pool(name="loads", bufs=4))
+        work = ctx.enter_context(tc.tile_pool(name="work", bufs=3))
+        resid = ctx.enter_context(tc.tile_pool(name="resid", bufs=4))
         stats = ctx.enter_context(tc.tile_pool(name="stats", bufs=4))
         psum_at = ctx.enter_context(tc.psum_pool(name="psum_at", bufs=2))
-        psum_mm = ctx.enter_context(tc.psum_pool(name="psum_mm", bufs=3))
-        psum_zt = ctx.enter_context(tc.psum_pool(name="psum_zt", bufs=Z_BANKS))
+        psum_mm = ctx.enter_context(tc.psum_pool(name="psum_mm", bufs=4))
+        psum_zt = ctx.enter_context(tc.psum_pool(name="psum_zt", bufs=2))
         ctx.enter_context(tc.manual_schedule())
 
-        gb_rows = keep.tile([P, P], BF16, name="gb_rows")
-        nc.vector.memset(gb_rows[:], 0.0)
+        live = {}
+
+        def load_attn(g):
+            if not 0 <= g < GROUPS:
+                return
+            attn_sb = loads.tile([P, QUAD, D], BF16, name="attn_sb")
+            nc.sync.dma_start(out=attn_sb[:], in_=quads(attn_flat, g * GROUP, GROUP))
+            live["attn_sb", g] = attn_sb
+
+        def load_x(g):
+            if not 0 <= g < GROUPS:
+                return
+            xm_sb = loads.tile([P, QUAD, D], BF16, name="xm_sb")
+            for first_p, n_p, first_token in image_pieces(g):
+                nc.sync.dma_start(out=xm_sb[first_p : first_p + n_p], in_=quads(x_flat, first_token, n_p * QUAD))
+            live["xm_sb", g] = xm_sb
+
         eps_col = keep.tile([P, 1], F32, name="eps_col")
         nc.vector.memset(eps_col[:], LN_EPS)
+        table_warm = keep.tile([P, 1], F32, name="table_warm")
+        nc.scalar.activation(out=table_warm[:], in_=eps_col[:], func=ACT.Abs_reciprocal_sqrt)
+        rows = keep.tile([P, D], BF16, name="rows")
+        nc.vector.memset(rows[:], 0.0)
 
+        load_attn(0)
         wo_raw = stage.tile([P, PACK, D], BF16, name="wo_raw")
         nc.sync.dma_start(out=wo_raw[:], in_=Wo2.rearrange("(p t) n -> p t n", t=PACK))
+        for r, vec in enumerate((bo2, bl, g4, b4)):
+            nc.sync.dma_start(out=rows[r : r + 1, :], in_=vec.rearrange("(o d) -> o d", o=1))
+        load_x(0)
         wl_raw = stage.tile([P, PACK, D], BF16, name="wl_raw")
         for t in range(PACK):
             nc.sync.dma_start(out=wl_raw[:, t, :], in_=Wl.rearrange("(b t r) n -> t b r n", t=PACK, r=RUN)[t])
-        for first, vec in ((0, g4), (PACK, b4)):
-            for t in range(PACK):
-                nc.scalar.dma_start(
-                    out=gb_rows[first + t : first + t + 1, :],
-                    in_=vec.rearrange("(o b t r) -> t o b r", o=1, t=PACK, r=RUN)[t],
-                )
-        bo2_all = keep.tile([P, D], BF16, name="bo2_all")
-        nc.scalar.dma_start(out=bo2_all[:], in_=bo2.partition_broadcast(P))
-        bl_all = keep.tile([P, D], BF16, name="bl_all")
-        nc.scalar.dma_start(out=bl_all[:], in_=bl.partition_broadcast(P))
+        load_attn(1)
 
         ident = keep.tile([P, P], F32, name="ident")
         make_identity(nc, ident[:])
@@ -106,233 +122,259 @@ def tile_successiveswintransfomerblock_pb_t_kernel(tc, attn_win, x_mid, Wo2, bo2
         rolled = to_image[:].rearrange("p (r m) -> p r m", m=ROW_QUADS)
         nc.vector.tensor_copy(out=rolled[:, :, 0 : ROW_QUADS - 1], in_=unrolled[:, :, 1:ROW_QUADS])
         nc.vector.tensor_copy(out=rolled[:, :, ROW_QUADS - 1 : ROW_QUADS], in_=unrolled[:, :, 0:1])
-
         ident_bf = keep.tile([P, P], BF16, name="ident_bf")
         nc.vector.tensor_copy(out=ident_bf[:], in_=ident[:])
 
-        wo_codes, wo_scales = quantise_weight(nc, stage, keep, wo_raw, "wo")
-        wl_codes, wl_scales = quantise_weight(nc, stage, keep, wl_raw, "wl")
 
-        gb_ps = psum_mm.tile([P, P], BF16, name="gb_ps", tag="acc")
-        nc.tensor.transpose(gb_ps[:], gb_rows[:], ident_bf[:])
-        gb_col = keep.tile([P, 2 * PACK], F32, name="gb_col")
-        nc.vector.tensor_copy(out=gb_col[:], in_=gb_ps[:, 0 : 2 * PACK])
+        def slots(u):
+            return slice(u % 2 * SLOTS, u % 2 * SLOTS + SLOTS)
 
-        live = {}
-
-        def load(g):
-            if not 0 <= g < GROUPS:
+        def attn_transpose(u):
+            if not 0 <= u < UNITS:
                 return
-            attn_sb = loads.tile([P, QUAD, D], BF16, name="attn_sb")
-            nc.sync.dma_start(out=attn_sb[:], in_=quads(attn_flat, g * GROUP, GROUP))
-            xm_sb = loads.tile([P, QUAD, D], BF16, name="xm_sb")
-            for first_p, n_p, first_token in image_pieces(g):
-                nc.sync.dma_start(out=xm_sb[first_p : first_p + n_p], in_=quads(x_flat, first_token, n_p * QUAD))
-            live["attn_sb", g] = attn_sb
-            live["xm_sb", g] = xm_sb
+            attn_words = live["attn_sb", u // 2][:, slots(u), :].bitcast(F32)
+            a_t = psum_at.tile([P, SLOTS, 2, P], F32, name="a_t")
+            for s in range(SLOTS):
+                for v in range(2):
+                    nc.tensor.transpose(a_t[:, s, v, :], attn_words[:, s, v : 2 * P : 2], to_image[:])
+            live["a_t", u] = a_t
 
-        def attn_transpose(g):
-            if not 0 <= g < GROUPS:
+        def attn_copy_out(u):
+            if not 0 <= u < UNITS:
                 return
-            attn_words = live["attn_sb", g][:].bitcast(F32)
-            for pair in range(QUAD // 2):
-                a_t = psum_at.tile([P, 2, 2, P], F32, name="a_t")
-                for s in range(2):
-                    for u in range(2):
-                        nc.tensor.transpose(
-                            a_t[:, s, u, :], attn_words[:, 2 * pair + s, u : 2 * P : 2], to_image[:]
-                        )
-                live["a_t", g, pair] = a_t
+            a_grouped = work.tile([P, SLOTS, P, PACK], BF16, name="a_grouped", align_bytes=64)
+            nc.scalar.copy(out=a_grouped[:].bitcast(F32), in_=live["a_t", u][:].rearrange("p s v r -> p s r v"))
+            live["a_grouped", u] = a_grouped
 
-        def attn_copy_out(g):
-            if not 0 <= g < GROUPS:
+        def quantise_attn(u):
+            if not 0 <= u < UNITS:
                 return
-            a_grouped = work.tile([P, QUAD, P, PACK], BF16, name="a_grouped", bufs=3, align_bytes=64)
-            for pair in range(QUAD // 2):
-                nc.scalar.copy(
-                    out=a_grouped[:, 2 * pair : 2 * pair + 2].bitcast(F32),
-                    in_=live["a_t", g, pair][:].rearrange("p s u r -> p s r u"),
-                )
-            live["a_grouped", g] = a_grouped
-
-        def quantise_attn(g):
-            if not 0 <= g < GROUPS:
-                return
-            a_codes = work.tile([P, GROUP], U32, name="a_codes", align_bytes=64)
-            a_scales = work.tile([P, GROUP], U8, name="a_scales", align_bytes=64)
+            a_codes = work.tile([P, UNIT], U32, name="a_codes", align_bytes=64)
+            a_scales = work.tile([P, UNIT], U8, name="a_scales", align_bytes=64)
             nc.vector.quantize_mx(
                 out=a_codes[:].bitcast(FP8X4),
                 scales=a_scales[:],
-                in_=live["a_grouped", g][:].rearrange("p q r t -> p (q r t)"),
+                in_=live["a_grouped", u][:].rearrange("p s r t -> p (s r t)"),
             )
-            live["a_codes", g] = a_codes
-            live["a_scales", g] = a_scales
+            live["a_codes", u] = a_codes
+            live["a_scales", u] = a_scales
 
-        def add_bo2(g):
-            if not 0 <= g < GROUPS:
+        def product(u, label, codes, scales):
+            if not 0 <= u < UNITS:
                 return
-            x = resid.tile([P, QUAD, D], F32, name="x")
-            nc.vector.tensor_tensor(
-                out=x[:], in0=live["xm_sb", g][:], in1=bo2_all[:].unsqueeze(1).to_broadcast([P, QUAD, D]), op=ADD
-            )
-            live["x", g] = x
-
-        def first_product(g):
-            if not 0 <= g < GROUPS:
-                return
-            x = live["x", g]
-            x_sum = stats.tile([P, QUAD], F32, name="x_sum")
-            for q in range(QUAD):
-                tokens = slice(q * P, (q + 1) * P)
-                acc1 = psum_mm.tile([P, D], F32, name="acc1", tag="acc")
+            for s in range(SLOTS):
+                tokens = slice(s * P, (s + 1) * P)
+                acc = psum_mm.tile([P, D], F32, name="acc")
                 nc.tensor.matmul_mx(
-                    out=acc1[:],
-                    lhsT=live["a_codes", g][:, tokens].bitcast(FP8X4),
-                    lhsT_scale=live["a_scales", g][:, tokens],
-                    rhs=wo_codes[:].bitcast(FP8X4),
-                    rhs_scale=wo_scales[:],
+                    out=acc[:],
+                    lhsT=live[label + "_codes", u][:, tokens].bitcast(FP8X4),
+                    lhsT_scale=live[label + "_scales", u][:, tokens],
+                    rhs=codes[:].bitcast(FP8X4),
+                    rhs_scale=scales[:],
                     start=True,
                     stop=True,
                 )
+                live[label + "_acc", u, s] = acc
+
+        def add_bo2(u):
+            if not 0 <= u < UNITS:
+                return
+            x = resid.tile([P, SLOTS, D], F32, name="x")
+            for s in range(SLOTS):
+                nc.gpsimd.tensor_tensor(
+                    out=x[:, s, :], in0=live["xm_sb", u // 2][:, u % 2 * SLOTS + s, :], in1=bo2_all[:], op=ADD
+                )
+            live["x", u] = x
+
+        def add_first_product(u):
+            if not 0 <= u < UNITS:
+                return
+            x = live["x", u]
+            x_sum = stats.tile([P, SLOTS], F32, name="x_sum")
+            for s in range(SLOTS):
                 nc.vector.scalar_tensor_tensor(
-                    out=x[:, q, :],
-                    in0=acc1[:],
+                    out=x[:, s, :],
+                    in0=live["a_acc", u, s][:],
                     scalar=1.0,
-                    in1=x[:, q, :],
+                    in1=x[:, s, :],
                     op0=MULT,
                     op1=ADD,
-                    accum_out=x_sum[:, q : q + 1],
+                    accum_out=x_sum[:, s : s + 1],
                 )
-            neg_mean = stats.tile([P, QUAD], F32, name="neg_mean")
-            nc.gpsimd.tensor_scalar(out=neg_mean[:], in0=x_sum[:], scalar1=-1.0 / D, scalar2=0.0, op0=MULT, op1=ADD)
-            live["neg_mean", g] = neg_mean
+            live["x_sum", u] = x_sum
 
-        def variance(g):
-            if not 0 <= g < GROUPS:
+        def squares(u, s):
+            if not 0 <= u < UNITS:
                 return
-            neg_mean = live["neg_mean", g]
-            sq_sum = stats.tile([P, QUAD], F32, name="sq_sum")
-            for q in range(QUAD):
-                squares = work.tile([P, D], BF16, name="squares")
-                nc.scalar.activation(
-                    out=squares[:],
-                    in_=live["x", g][:, q, :],
-                    func=ACT.Square,
-                    bias=neg_mean[:, q : q + 1],
-                    scale=1.0,
-                    accum_out=sq_sum[:, q : q + 1],
-                )
-            rstd = stats.tile([P, QUAD], F32, name="rstd")
+            if s == 0:
+                live["sq_sum", u] = stats.tile([P, SLOTS], F32, name="sq_sum")
+            junk = work.tile([P, D], BF16, name="junk")
             nc.scalar.activation(
-                out=rstd[:], in_=sq_sum[:], func=ACT.Abs_reciprocal_sqrt, bias=eps_col[:], scale=1.0 / D
+                out=junk[:],
+                in_=live["x", u][:, s, :],
+                func=ACT.Square,
+                bias=live["x_sum", u][:, s : s + 1],
+                scale=-float(D),
+                accum_out=live["sq_sum", u][:, s : s + 1],
             )
-            shift = stats.tile([P, QUAD], F32, name="shift")
-            nc.gpsimd.tensor_tensor(out=shift[:], in0=neg_mean[:], in1=rstd[:], op=MULT)
-            live["rstd", g] = rstd
-            live["shift", g] = shift
 
-        def normalise(g):
-            if not 0 <= g < GROUPS:
+        def inverse_deviation(u):
+            if not 0 <= u < UNITS:
                 return
-            z = work.tile([P, QUAD, D], F32, name="z")
-            for q in range(QUAD):
+            rstd = stats.tile([P, SLOTS], F32, name="rstd")
+            nc.scalar.activation(
+                out=rstd[:],
+                in_=live["sq_sum", u][:],
+                func=ACT.Abs_reciprocal_sqrt,
+                bias=eps_col[:],
+                scale=1.0 / (D * D * D),
+            )
+            live["rstd", u] = rstd
+
+        def norm_shift(u):
+            if not 0 <= u < UNITS:
+                return
+            shift = stats.tile([P, SLOTS], F32, name="shift")
+            nc.vector.scalar_tensor_tensor(
+                out=shift[:], in0=live["x_sum", u][:], scalar=-1.0 / D, in1=live["rstd", u][:], op0=MULT, op1=MULT
+            )
+            live["shift", u] = shift
+
+        def normalise(u):
+            if not 0 <= u < UNITS:
+                return
+            z = work.tile([P, SLOTS, D], F32, name="z")
+            for s in range(SLOTS):
                 nc.scalar.activation(
-                    out=z[:, q, :].rearrange("p (t b r) -> p t b r", t=PACK, r=RUN),
-                    in_=live["x", g][:, q, :].rearrange("p (b t r) -> p t b r", t=PACK, r=RUN),
+                    out=z[:, s, :].rearrange("p (t b r) -> p t b r", t=PACK, r=RUN),
+                    in_=live["x", u][:, s, :].rearrange("p (b t r) -> p t b r", t=PACK, r=RUN),
                     func=ACT.Identity,
-                    bias=live["shift", g][:, q : q + 1],
-                    scale=live["rstd", g][:, q : q + 1],
+                    bias=live["shift", u][:, s : s + 1],
+                    scale=live["rstd", u][:, s : s + 1],
                 )
-            live["z", g] = z
+            live["z", u] = z
 
-        def z_transpose(g, t):
-            if not 0 <= g < GROUPS:
+        def z_transpose(u):
+            if not 0 <= u < UNITS:
                 return
-            z_t = psum_zt.tile([P, GROUP], F32, name="z_t")
-            for q in range(QUAD):
-                nc.tensor.transpose(z_t[:, q * P : (q + 1) * P], live["z", g][:, q, t * P : (t + 1) * P], ident[:])
-            live["z_t", g, t] = z_t
+            banks = []
+            for half in range(2):
+                z_t = psum_zt.tile([P, 2, UNIT], F32, name="z_t")
+                banks.append(z_t)
+            for s in range(SLOTS):
+                for t in range(PACK):
+                    nc.tensor.transpose(
+                        banks[t // 2][:, t % 2, s * P : (s + 1) * P], live["z", u][:, s, t * P : (t + 1) * P], ident[:]
+                    )
+            live["z_t", u] = banks
 
-        def gain_and_bias(g, t):
-            if not 0 <= g < GROUPS:
+        def gain_and_bias(u):
+            if not 0 <= u < UNITS:
                 return
-            if t == 0:
-                live["h_t", g] = work.tile([P, PACK, GROUP], BF16, name="h_t")
-            nc.scalar.activation(
-                out=live["h_t", g][:, t, :],
-                in_=live["z_t", g, t][:],
-                func=ACT.Identity,
-                bias=gb_col[:, PACK + t : PACK + t + 1],
-                scale=gb_col[:, t : t + 1],
-            )
+            h_t = work.tile([P, PACK, UNIT], BF16, name="h_t")
+            for t in range(PACK):
+                nc.scalar.activation(
+                    out=h_t[:, t, :],
+                    in_=live["z_t", u][t // 2][:, t % 2, :],
+                    func=ACT.Identity,
+                    bias=b_col[:, t : t + 1],
+                    scale=g_col[:, t : t + 1],
+                )
+            live["h_t", u] = h_t
 
-        def regroup_h(g):
-            if not 0 <= g < GROUPS:
+        def regroup_h(u):
+            if not 0 <= u < UNITS:
                 return
-            h_grouped = work.tile([P, GROUP, PACK], BF16, name="h_grouped", align_bytes=64)
-            nc.scalar.copy(
+            h_grouped = work.tile([P, UNIT, PACK], BF16, name="h_grouped", align_bytes=64)
+            nc.vector.tensor_copy(
                 out=h_grouped[:].rearrange("p (c i) t -> p c t i", i=4),
-                in_=live["h_t", g][:].rearrange("p t (c i) -> p c t i", i=4),
+                in_=live["h_t", u][:].rearrange("p t (c i) -> p c t i", i=4),
             )
-            live["h_grouped", g] = h_grouped
+            live["h_grouped", u] = h_grouped
 
-        def quantise_h(g):
-            if not 0 <= g < GROUPS:
+        def quantise_h(u):
+            if not 0 <= u < UNITS:
                 return
-            h_codes = work.tile([P, GROUP], U32, name="h_codes", align_bytes=64)
-            h_scales = work.tile([P, GROUP], U8, name="h_scales", align_bytes=64)
+            h_codes = work.tile([P, UNIT], U32, name="h_codes", align_bytes=64)
+            h_scales = work.tile([P, UNIT], U8, name="h_scales", align_bytes=64)
             nc.vector.quantize_mx(
                 out=h_codes[:].bitcast(FP8X4),
                 scales=h_scales[:],
-                in_=live["h_grouped", g][:].rearrange("p r t -> p (r t)"),
+                in_=live["h_grouped", u][:].rearrange("p r t -> p (r t)"),
             )
-            live["h_codes", g] = h_codes
-            live["h_scales", g] = h_scales
+            live["h_codes", u] = h_codes
+            live["h_scales", u] = h_scales
 
-        def add_bl(g):
-            if not 0 <= g < GROUPS:
+        def add_bl(u):
+            if not 0 <= u < UNITS:
                 return
-            x = live["x", g]
-            nc.vector.tensor_tensor(out=x[:], in0=x[:], in1=bl_all[:].unsqueeze(1).to_broadcast([P, QUAD, D]), op=ADD)
+            y = resid.tile([P, SLOTS, D], F32, name="y")
+            nc.vector.tensor_tensor(
+                out=y[:], in0=live["x", u][:], in1=bl_all[:].unsqueeze(1).to_broadcast([P, SLOTS, D]), op=ADD
+            )
+            live["y", u] = y
 
-        def second_product(g):
-            if not 0 <= g < GROUPS:
+        def add_second_product(u):
+            if not 0 <= u < UNITS:
                 return
-            x = live["x", g]
-            for q in range(QUAD):
-                tokens = slice(q * P, (q + 1) * P)
-                acc2 = psum_mm.tile([P, D], F32, name="acc2", tag="acc")
-                nc.tensor.matmul_mx(
-                    out=acc2[:],
-                    lhsT=live["h_codes", g][:, tokens].bitcast(FP8X4),
-                    lhsT_scale=live["h_scales", g][:, tokens],
-                    rhs=wl_codes[:].bitcast(FP8X4),
-                    rhs_scale=wl_scales[:],
-                    start=True,
-                    stop=True,
+            y = live["y", u]
+            for s in range(SLOTS):
+                nc.vector.tensor_tensor(out=y[:, s, :], in0=live["h_acc", u, s][:], in1=y[:, s, :], op=ADD)
+            for first_p, n_p, first_token in image_pieces(u // 2):
+                nc.sync.dma_start(
+                    out=quads(out_flat, first_token, n_p * QUAD)[:, slots(u), :], in_=y[first_p : first_p + n_p]
                 )
-                nc.vector.tensor_tensor(out=x[:, q, :], in0=acc2[:], in1=x[:, q, :], op=ADD)
-                for first_p, n_p, first_token in image_pieces(g):
-                    nc.sync.dma_start(
-                        out=quads(out_flat, first_token, n_p * QUAD)[:, q, :], in_=x[first_p : first_p + n_p, q, :]
-                    )
 
-        for step in range(-3, GROUPS + 2):
-            load(step + 3)
-            attn_transpose(step + 2)
-            quantise_h(step - 2)
-            add_bl(step - 1)
-            variance(step)
-            quantise_attn(step + 1)
-            attn_copy_out(step + 2)
-            second_product(step - 2)
-            first_product(step + 1)
-            add_bo2(step + 2)
-            normalise(step)
+        wo_codes, wo_scales = quantise_weight(nc, stage, keep, wo_raw, "wo")
+
+        bias_all = []
+        for r, label in enumerate(("bo2_all", "bl_all")):
+            spread = psum_mm.tile([P, D], F32, name="spread", tag="acc")
+            nc.tensor.matmul(
+                spread[:], lhsT=ident_bf[:, r : r + 1].to_broadcast([P, P]), rhs=rows[:], start=True, stop=True
+            )
+            everywhere = keep.tile([P, D], BF16, name=label)
+            nc.scalar.copy(out=everywhere[:], in_=spread[:])
+            bias_all.append(everywhere)
+        bo2_all, bl_all = bias_all
+
+        rows_by_t = keep.tile([P, PACK, P], BF16, name="rows_by_t")
+        nc.vector.tensor_copy(
+            out=rows_by_t[:].rearrange("p t (b r) -> p t b r", r=RUN),
+            in_=rows[:].rearrange("p (b t r) -> p t b r", t=PACK, r=RUN),
+        )
+        gb_ps = psum_mm.tile([P, PACK, P], BF16, name="gb_ps", tag="acc")
+        for t in range(PACK):
+            nc.tensor.transpose(gb_ps[:, t, :], rows_by_t[:, t, :], ident_bf[:])
+        g_col = keep.tile([P, PACK], F32, name="g_col")
+        nc.vector.tensor_copy(out=g_col[:], in_=gb_ps[:, :, 2])
+        b_col = keep.tile([P, PACK], F32, name="b_col")
+        nc.vector.tensor_copy(out=b_col[:], in_=gb_ps[:, :, 3])
+
+        wl_codes, wl_scales = quantise_weight(nc, stage, keep, wl_raw, "wl")
+
+        for step in range(-4, UNITS + 2):
+            if step % 2 == 0:
+                group = (step + 8) // 2
+                if group >= 2:
+                    load_attn(group)
+                if group >= 2:
+                    load_x(group - 1)
+            attn_transpose(step + 4)
+            add_first_product(step + 1)
+            add_second_product(step - 2)
+            squares(step, 0)
+            gain_and_bias(step - 1)
+            squares(step, 1)
+            inverse_deviation(step)
+            attn_copy_out(step + 3)
             regroup_h(step - 1)
-            for t in range(Z_BANKS):
-                z_transpose(step, t)
-            for t in range(PACK):
-                gain_and_bias(step, t)
-                if t + Z_BANKS < PACK:
-                    z_transpose(step, t + Z_BANKS)
+            norm_shift(step)
+            quantise_attn(step + 2)
+            product(step + 2, "a", wo_codes, wo_scales)
+            quantise_h(step - 1)
+            add_bl(step - 1)
+            normalise(step)
+            z_transpose(step)
+            product(step - 1, "h", wl_codes, wl_scales)
+            add_bo2(step + 2)

@@ -70,7 +70,8 @@ def tile_successiveswintransfomerblock_pb_t_kernel(tc, attn_win, x_mid, Wo2, bo2
         work = ctx.enter_context(tc.tile_pool(name="work", bufs=3))
         resid = ctx.enter_context(tc.tile_pool(name="resid", bufs=4))
         stats = ctx.enter_context(tc.tile_pool(name="stats", bufs=4))
-        psum_at = ctx.enter_context(tc.psum_pool(name="psum_at", bufs=2))
+        psum_keep = ctx.enter_context(tc.psum_pool(name="psum_keep", bufs=1))
+        psum_at = ctx.enter_context(tc.psum_pool(name="psum_at", bufs=1))
         psum_mm = ctx.enter_context(tc.psum_pool(name="psum_mm", bufs=4))
         psum_zt = ctx.enter_context(tc.psum_pool(name="psum_zt", bufs=2))
         ctx.enter_context(tc.manual_schedule())
@@ -81,7 +82,11 @@ def tile_successiveswintransfomerblock_pb_t_kernel(tc, attn_win, x_mid, Wo2, bo2
             if not 0 <= g < GROUPS:
                 return
             attn_sb = loads.tile([P, QUAD, D], BF16, name="attn_sb")
-            nc.sync.dma_start(out=attn_sb[:], in_=quads(attn_flat, g * GROUP, GROUP))
+            source = quads(attn_flat, g * GROUP, GROUP)
+            pieces = 2 if g == 0 else 1
+            for i in range(pieces):
+                part = slice(i * QUAD // pieces, (i + 1) * QUAD // pieces)
+                nc.sync.dma_start(out=attn_sb[:, part, :], in_=source[:, part, :])
             live["attn_sb", g] = attn_sb
 
         def load_x(g):
@@ -99,16 +104,16 @@ def tile_successiveswintransfomerblock_pb_t_kernel(tc, attn_win, x_mid, Wo2, bo2
         rows = keep.tile([P, D], BF16, name="rows")
         nc.vector.memset(rows[:], 0.0)
 
+        for r, vec in enumerate((bo2, bl, g4, b4)):
+            nc.sync.dma_start(out=rows[r : r + 1, :], in_=vec.rearrange("(o d) -> o d", o=1))
         load_attn(0)
         wo_raw = stage.tile([P, PACK, D], BF16, name="wo_raw")
         nc.sync.dma_start(out=wo_raw[:], in_=Wo2.rearrange("(p t) n -> p t n", t=PACK))
-        for r, vec in enumerate((bo2, bl, g4, b4)):
-            nc.sync.dma_start(out=rows[r : r + 1, :], in_=vec.rearrange("(o d) -> o d", o=1))
         load_x(0)
+        load_attn(1)
         wl_raw = stage.tile([P, PACK, D], BF16, name="wl_raw")
         for t in range(PACK):
             nc.sync.dma_start(out=wl_raw[:, t, :], in_=Wl.rearrange("(b t r) n -> t b r n", t=PACK, r=RUN)[t])
-        load_attn(1)
 
         ident = keep.tile([P, P], F32, name="ident")
         make_identity(nc, ident[:])
@@ -179,24 +184,25 @@ def tile_successiveswintransfomerblock_pb_t_kernel(tc, attn_win, x_mid, Wo2, bo2
         def add_bo2(u):
             if not 0 <= u < UNITS:
                 return
-            x = resid.tile([P, SLOTS, D], F32, name="x")
+            engine = nc.vector if u == 0 else nc.gpsimd
             for s in range(SLOTS):
-                nc.gpsimd.tensor_tensor(
-                    out=x[:, s, :], in0=live["xm_sb", u // 2][:, u % 2 * SLOTS + s, :], in1=bo2_all[:], op=ADD
+                x = resid.tile([P, D], F32, name="x", tag="x%d" % s, bufs=3 + s)
+                engine.tensor_tensor(
+                    out=x[:], in0=live["xm_sb", u // 2][:, u % 2 * SLOTS + s, :], in1=bo2_all[:], op=ADD
                 )
-            live["x", u] = x
+                live["x", u, s] = x
 
         def add_first_product(u):
             if not 0 <= u < UNITS:
                 return
-            x = live["x", u]
             x_sum = stats.tile([P, SLOTS], F32, name="x_sum")
             for s in range(SLOTS):
+                x = live["x", u, s]
                 nc.vector.scalar_tensor_tensor(
-                    out=x[:, s, :],
+                    out=x[:],
                     in0=live["a_acc", u, s][:],
                     scalar=1.0,
-                    in1=x[:, s, :],
+                    in1=x[:],
                     op0=MULT,
                     op1=ADD,
                     accum_out=x_sum[:, s : s + 1],
@@ -211,7 +217,7 @@ def tile_successiveswintransfomerblock_pb_t_kernel(tc, attn_win, x_mid, Wo2, bo2
             junk = work.tile([P, D], BF16, name="junk")
             nc.scalar.activation(
                 out=junk[:],
-                in_=live["x", u][:, s, :],
+                in_=live["x", u, s][:],
                 func=ACT.Square,
                 bias=live["x_sum", u][:, s : s + 1],
                 scale=-float(D),
@@ -247,7 +253,7 @@ def tile_successiveswintransfomerblock_pb_t_kernel(tc, attn_win, x_mid, Wo2, bo2
             for s in range(SLOTS):
                 nc.scalar.activation(
                     out=z[:, s, :].rearrange("p (t b r) -> p t b r", t=PACK, r=RUN),
-                    in_=live["x", u][:, s, :].rearrange("p (b t r) -> p t b r", t=PACK, r=RUN),
+                    in_=live["x", u, s][:].rearrange("p (b t r) -> p t b r", t=PACK, r=RUN),
                     func=ACT.Identity,
                     bias=live["shift", u][:, s : s + 1],
                     scale=live["rstd", u][:, s : s + 1],
@@ -305,14 +311,12 @@ def tile_successiveswintransfomerblock_pb_t_kernel(tc, attn_win, x_mid, Wo2, bo2
             live["h_codes", u] = h_codes
             live["h_scales", u] = h_scales
 
-        def add_bl(u):
+        def add_bl(u, s):
             if not 0 <= u < UNITS:
                 return
-            y = resid.tile([P, SLOTS, D], F32, name="y")
-            nc.vector.tensor_tensor(
-                out=y[:], in0=live["x", u][:], in1=bl_all[:].unsqueeze(1).to_broadcast([P, SLOTS, D]), op=ADD
-            )
-            live["y", u] = y
+            if s == 0:
+                live["y", u] = resid.tile([P, SLOTS, D], F32, name="y")
+            nc.vector.tensor_tensor(out=live["y", u][:, s, :], in0=bl_all[:], in1=live["x", u, s][:], op=ADD)
 
         def add_second_product(u):
             if not 0 <= u < UNITS:
@@ -325,18 +329,19 @@ def tile_successiveswintransfomerblock_pb_t_kernel(tc, attn_win, x_mid, Wo2, bo2
                     out=quads(out_flat, first_token, n_p * QUAD)[:, slots(u), :], in_=y[first_p : first_p + n_p]
                 )
 
-        wo_codes, wo_scales = quantise_weight(nc, stage, keep, wo_raw, "wo")
-
-        bias_all = []
-        for r, label in enumerate(("bo2_all", "bl_all")):
-            spread = psum_mm.tile([P, D], F32, name="spread", tag="acc")
+        attn_transpose(0)
+        attn_copy_out(0)
+        def spread(target, r):
             nc.tensor.matmul(
-                spread[:], lhsT=ident_bf[:, r : r + 1].to_broadcast([P, P]), rhs=rows[:], start=True, stop=True
+                target[:], lhsT=ident_bf[:, r : r + 1].to_broadcast([P, P]), rhs=rows[:], start=True, stop=True
             )
-            everywhere = keep.tile([P, D], BF16, name=label)
-            nc.scalar.copy(out=everywhere[:], in_=spread[:])
-            bias_all.append(everywhere)
-        bo2_all, bl_all = bias_all
+
+        bo2_ps = psum_mm.tile([P, D], F32, name="bo2_ps", tag="acc")
+        spread(bo2_ps, 0)
+        bo2_all = keep.tile([P, D], BF16, name="bo2_all")
+        nc.scalar.copy(out=bo2_all[:], in_=bo2_ps[:])
+        bl_all = psum_keep.tile([P, D], F32, name="bl_all")
+        spread(bl_all, 1)
 
         rows_by_t = keep.tile([P, PACK, P], BF16, name="rows_by_t")
         nc.vector.tensor_copy(
@@ -351,30 +356,39 @@ def tile_successiveswintransfomerblock_pb_t_kernel(tc, attn_win, x_mid, Wo2, bo2
         b_col = keep.tile([P, PACK], F32, name="b_col")
         nc.vector.tensor_copy(out=b_col[:], in_=gb_ps[:, :, 3])
 
-        wl_codes, wl_scales = quantise_weight(nc, stage, keep, wl_raw, "wl")
+        wo_codes, wo_scales = quantise_weight(nc, stage, keep, wo_raw, "wo")
+        quantise_attn(0)
+        attn_transpose(1)
+        attn_copy_out(1)
+        add_bo2(0)
+        product(0, "a", wo_codes, wo_scales)
+        attn_transpose(2)
+        load_attn(2)
+        load_x(1)
 
-        for step in range(-4, UNITS + 2):
+        for step in range(-1, UNITS + 2):
             if step % 2 == 0:
-                group = (step + 8) // 2
-                if group >= 2:
-                    load_attn(group)
-                if group >= 2:
-                    load_x(group - 1)
-            attn_transpose(step + 4)
+                load_attn((step + 6) // 2)
+                load_x((step + 4) // 2)
+            add_bl(step - 1, 0)
+            add_bo2(step + 2)
             add_first_product(step + 1)
             add_second_product(step - 2)
+            add_bl(step - 1, 1)
             squares(step, 0)
             gain_and_bias(step - 1)
             squares(step, 1)
             inverse_deviation(step)
             attn_copy_out(step + 3)
-            regroup_h(step - 1)
+            attn_transpose(step + 4)
             norm_shift(step)
+            regroup_h(step - 1)
             quantise_attn(step + 2)
+            if step == 0:
+                wl_codes, wl_scales = quantise_weight(nc, stage, keep, wl_raw, "wl")
             product(step + 2, "a", wo_codes, wo_scales)
             quantise_h(step - 1)
-            add_bl(step - 1)
             normalise(step)
             z_transpose(step)
-            product(step - 1, "h", wl_codes, wl_scales)
-            add_bo2(step + 2)
+            if step > 0:
+                product(step - 1, "h", wl_codes, wl_scales)

@@ -186,7 +186,7 @@ def tile_successiveswintransfomerblock_pb_t_kernel(tc, attn_win, x_mid, Wo2, bo2
                 return
             engine = nc.vector if u == 0 else nc.gpsimd
             for s in range(SLOTS):
-                x = resid.tile([P, D], F32, name="x", tag="x%d" % s, bufs=3 + s)
+                x = resid.tile([P, D], F32, name="x", tag="x%d" % s, bufs=4 + s)
                 engine.tensor_tensor(
                     out=x[:], in0=live["xm_sb", u // 2][:, u % 2 * SLOTS + s, :], in1=bo2_all[:], op=ADD
                 )
@@ -329,8 +329,6 @@ def tile_successiveswintransfomerblock_pb_t_kernel(tc, attn_win, x_mid, Wo2, bo2
                     out=quads(out_flat, first_token, n_p * QUAD)[:, slots(u), :], in_=y[first_p : first_p + n_p]
                 )
 
-        attn_transpose(0)
-        attn_copy_out(0)
         def spread(target, r):
             nc.tensor.matmul(
                 target[:], lhsT=ident_bf[:, r : r + 1].to_broadcast([P, P]), rhs=rows[:], start=True, stop=True
@@ -340,9 +338,19 @@ def tile_successiveswintransfomerblock_pb_t_kernel(tc, attn_win, x_mid, Wo2, bo2
         spread(bo2_ps, 0)
         bo2_all = keep.tile([P, D], BF16, name="bo2_all")
         nc.scalar.copy(out=bo2_all[:], in_=bo2_ps[:])
+        attn_transpose(0)
+        attn_copy_out(0)
+        wo_codes, wo_scales = quantise_weight(nc, stage, keep, wo_raw, "wo")
+        quantise_attn(0)
+        attn_transpose(1)
+        attn_copy_out(1)
+        add_bo2(0)
+        product(0, "a", wo_codes, wo_scales)
         bl_all = psum_keep.tile([P, D], F32, name="bl_all")
         spread(bl_all, 1)
-
+        attn_transpose(2)
+        load_attn(2)
+        load_x(1)
         rows_by_t = keep.tile([P, PACK, P], BF16, name="rows_by_t")
         nc.vector.tensor_copy(
             out=rows_by_t[:].rearrange("p t (b r) -> p t b r", r=RUN),
@@ -356,39 +364,29 @@ def tile_successiveswintransfomerblock_pb_t_kernel(tc, attn_win, x_mid, Wo2, bo2
         b_col = keep.tile([P, PACK], F32, name="b_col")
         nc.vector.tensor_copy(out=b_col[:], in_=gb_ps[:, :, 3])
 
-        wo_codes, wo_scales = quantise_weight(nc, stage, keep, wo_raw, "wo")
-        quantise_attn(0)
-        attn_transpose(1)
-        attn_copy_out(1)
-        add_bo2(0)
-        product(0, "a", wo_codes, wo_scales)
-        attn_transpose(2)
-        load_attn(2)
-        load_x(1)
-
-        for step in range(-1, UNITS + 2):
+        for step in range(-1, UNITS + 3):
             if step % 2 == 0:
                 load_attn((step + 6) // 2)
                 load_x((step + 4) // 2)
-            add_bl(step - 1, 0)
+            add_bl(step - 2, 0)
+            add_bl(step - 2, 1)
             add_bo2(step + 2)
             add_first_product(step + 1)
-            add_second_product(step - 2)
-            add_bl(step - 1, 1)
+            add_second_product(step - 3)
+            normalise(step - 1)
+            z_transpose(step - 1)
             squares(step, 0)
-            gain_and_bias(step - 1)
             squares(step, 1)
             inverse_deviation(step)
             attn_copy_out(step + 3)
             attn_transpose(step + 4)
-            norm_shift(step)
-            regroup_h(step - 1)
+            gain_and_bias(step - 1)
+            regroup_h(step - 2)
             quantise_attn(step + 2)
+            norm_shift(step)
+            product(step + 2, "a", wo_codes, wo_scales)
             if step == 0:
                 wl_codes, wl_scales = quantise_weight(nc, stage, keep, wl_raw, "wl")
-            product(step + 2, "a", wo_codes, wo_scales)
-            quantise_h(step - 1)
-            normalise(step)
-            z_transpose(step)
+            quantise_h(step - 2)
             if step > 0:
-                product(step - 1, "h", wl_codes, wl_scales)
+                product(step - 2, "h", wl_codes, wl_scales)

@@ -29,6 +29,7 @@ IMAGE_TOKENS = WINDOW_ROWS * GROUP
 ROW_QUADS = 16
 SHIFT_TOKENS = GROUP // 2
 LN_EPS = 1e-5
+SCALAR_TOKENS = 96
 
 FLOPS = 2 * 2 * IMAGES * IMAGE_TOKENS * D * D
 
@@ -288,15 +289,17 @@ def tile_successiveswintransfomerblock_pb_t_kernel(tc, attn_win, x_mid, Wo2, bo2
                 )
             live["h_t", u] = h_t
 
-        def regroup_h(u):
+        def regroup_h(u, engine):
             if not 0 <= u < UNITS:
                 return
-            h_grouped = work.tile([P, UNIT, PACK], BF16, name="h_grouped", align_bytes=64)
-            nc.vector.tensor_copy(
-                out=h_grouped[:].rearrange("p (c i) t -> p c t i", i=4),
-                in_=live["h_t", u][:].rearrange("p t (c i) -> p c t i", i=4),
+            if engine == nc.scalar:
+                live["h_grouped", u] = work.tile([P, UNIT, PACK], BF16, name="h_grouped", align_bytes=64)
+            tokens = slice(0, SCALAR_TOKENS) if engine == nc.scalar else slice(SCALAR_TOKENS, UNIT)
+            copy = nc.scalar.copy if engine == nc.scalar else nc.vector.tensor_copy
+            copy(
+                out=live["h_grouped", u][:, tokens, :].rearrange("p (c i) t -> p c t i", i=4),
+                in_=live["h_t", u][:, :, tokens].rearrange("p t (c i) -> p c t i", i=4),
             )
-            live["h_grouped", u] = h_grouped
 
         def quantise_h(u):
             if not 0 <= u < UNITS:
@@ -377,11 +380,12 @@ def tile_successiveswintransfomerblock_pb_t_kernel(tc, attn_win, x_mid, Wo2, bo2
             z_transpose(step - 1)
             squares(step, 0)
             squares(step, 1)
-            inverse_deviation(step)
             attn_copy_out(step + 3)
             attn_transpose(step + 4)
+            inverse_deviation(step)
+            regroup_h(step - 2, nc.scalar)
             gain_and_bias(step - 1)
-            regroup_h(step - 2)
+            regroup_h(step - 2, nc.vector)
             quantise_attn(step + 2)
             norm_shift(step)
             product(step + 2, "a", wo_codes, wo_scales)

@@ -29,6 +29,7 @@ IMAGE_TOKENS = WINDOW_ROWS * GROUP
 ROW_QUADS = 16
 SHIFT_TOKENS = GROUP // 2
 LN_EPS = 1e-5
+EARLY = 2
 SCALAR_TOKENS = 96
 
 FLOPS = 2 * 2 * IMAGES * IMAGE_TOKENS * D * D
@@ -47,9 +48,13 @@ def image_pieces(g):
     return [(0, P, base + window_row * GROUP - SHIFT_TOKENS)]
 
 
-def quantise_weight(nc, stage, keep, raw, label):
+def regroup_weight(nc, stage, raw, label):
     grouped = stage.tile([P, D, PACK], BF16, name="grouped_" + label, align_bytes=64)
     nc.vector.tensor_copy(out=grouped[:], in_=raw[:].rearrange("p t n -> p n t"))
+    return grouped
+
+
+def quantise_weight(nc, keep, grouped, label):
     codes = keep.tile([P, D], U32, name="codes_" + label, align_bytes=64)
     scales = keep.tile([P, D], U8, name="scales_" + label, align_bytes=64)
     nc.vector.quantize_mx(
@@ -79,16 +84,13 @@ def tile_successiveswintransfomerblock_pb_t_kernel(tc, attn_win, x_mid, Wo2, bo2
 
         live = {}
 
-        def load_attn(g):
+        def load_attn(g, half=None):
             if not 0 <= g < GROUPS:
                 return
-            attn_sb = loads.tile([P, QUAD, D], BF16, name="attn_sb")
-            source = quads(attn_flat, g * GROUP, GROUP)
-            pieces = 2 if g == 0 else 1
-            for i in range(pieces):
-                part = slice(i * QUAD // pieces, (i + 1) * QUAD // pieces)
-                nc.sync.dma_start(out=attn_sb[:, part, :], in_=source[:, part, :])
-            live["attn_sb", g] = attn_sb
+            if half != 1:
+                live["attn_sb", g] = loads.tile([P, QUAD, D], BF16, name="attn_sb")
+            part = slice(0, QUAD) if half is None else slice(half * SLOTS, half * SLOTS + SLOTS)
+            nc.sync.dma_start(out=live["attn_sb", g][:, part, :], in_=quads(attn_flat, g * GROUP, GROUP)[:, part, :])
 
         def load_x(g):
             if not 0 <= g < GROUPS:
@@ -105,11 +107,12 @@ def tile_successiveswintransfomerblock_pb_t_kernel(tc, attn_win, x_mid, Wo2, bo2
         rows = keep.tile([P, D], BF16, name="rows")
         nc.vector.memset(rows[:], 0.0)
 
-        for r, vec in enumerate((bo2, bl, g4, b4)):
-            nc.sync.dma_start(out=rows[r : r + 1, :], in_=vec.rearrange("(o d) -> o d", o=1))
-        load_attn(0)
+        load_attn(0, 0)
         wo_raw = stage.tile([P, PACK, D], BF16, name="wo_raw")
         nc.sync.dma_start(out=wo_raw[:], in_=Wo2.rearrange("(p t) n -> p t n", t=PACK))
+        for r, vec in enumerate((bo2, bl, g4, b4)):
+            nc.sync.dma_start(out=rows[r : r + 1, :], in_=vec.rearrange("(o d) -> o d", o=1))
+        load_attn(0, 1)
         load_x(0)
         load_attn(1)
         wl_raw = stage.tile([P, PACK, D], BF16, name="wl_raw")
@@ -185,11 +188,15 @@ def tile_successiveswintransfomerblock_pb_t_kernel(tc, attn_win, x_mid, Wo2, bo2
         def add_bo2(u):
             if not 0 <= u < UNITS:
                 return
-            engine = nc.vector if u == 0 else nc.gpsimd
             for s in range(SLOTS):
+                early = u < EARLY
+                engine = nc.vector if early else nc.gpsimd
                 x = resid.tile([P, D], F32, name="x", tag="x%d" % s, bufs=4 + s)
                 engine.tensor_tensor(
-                    out=x[:], in0=live["xm_sb", u // 2][:, u % 2 * SLOTS + s, :], in1=bo2_all[:], op=ADD
+                    out=x[:],
+                    in0=bo2_ps[:] if early else bo2_all[:],
+                    in1=live["xm_sb", u // 2][:, u % 2 * SLOTS + s, :],
+                    op=ADD,
                 )
                 live["x", u, s] = x
 
@@ -325,12 +332,17 @@ def tile_successiveswintransfomerblock_pb_t_kernel(tc, attn_win, x_mid, Wo2, bo2
             if not 0 <= u < UNITS:
                 return
             y = live["y", u]
+            pieces = SLOTS if u == UNITS - 1 else 1
             for s in range(SLOTS):
                 nc.vector.tensor_tensor(out=y[:, s, :], in0=live["h_acc", u, s][:], in1=y[:, s, :], op=ADD)
-            for first_p, n_p, first_token in image_pieces(u // 2):
-                nc.sync.dma_start(
-                    out=quads(out_flat, first_token, n_p * QUAD)[:, slots(u), :], in_=y[first_p : first_p + n_p]
-                )
+                if (s + 1) % (SLOTS // pieces) == 0:
+                    done = slice(s + 1 - SLOTS // pieces, s + 1)
+                    in_quad = slice(slots(u).start + done.start, slots(u).start + done.stop)
+                    for first_p, n_p, first_token in image_pieces(u // 2):
+                        nc.sync.dma_start(
+                            out=quads(out_flat, first_token, n_p * QUAD)[:, in_quad, :],
+                            in_=y[first_p : first_p + n_p, done, :],
+                        )
 
         def spread(target, r):
             nc.tensor.matmul(
@@ -340,42 +352,37 @@ def tile_successiveswintransfomerblock_pb_t_kernel(tc, attn_win, x_mid, Wo2, bo2
         bo2_ps = psum_mm.tile([P, D], F32, name="bo2_ps", tag="acc")
         spread(bo2_ps, 0)
         bo2_all = keep.tile([P, D], BF16, name="bo2_all")
-        nc.scalar.copy(out=bo2_all[:], in_=bo2_ps[:])
         attn_transpose(0)
         attn_copy_out(0)
-        wo_codes, wo_scales = quantise_weight(nc, stage, keep, wo_raw, "wo")
+        wo_grouped = regroup_weight(nc, stage, wo_raw, "wo")
         quantise_attn(0)
+        wo_codes, wo_scales = quantise_weight(nc, keep, wo_grouped, "wo")
         attn_transpose(1)
         attn_copy_out(1)
-        add_bo2(0)
         product(0, "a", wo_codes, wo_scales)
+        add_bo2(0)
+        quantise_attn(1)
+        attn_transpose(2)
+        nc.scalar.copy(out=bo2_all[:], in_=bo2_ps[:])
+        attn_copy_out(2)
+        product(1, "a", wo_codes, wo_scales)
+        add_first_product(0)
+        add_bo2(1)
+        load_x(1)
+        load_attn(2)
+        add_bo2(2)
+        attn_transpose(3)
         bl_all = psum_keep.tile([P, D], F32, name="bl_all")
         spread(bl_all, 1)
-        attn_transpose(2)
-        load_attn(2)
-        load_x(1)
-        rows_by_t = keep.tile([P, PACK, P], BF16, name="rows_by_t")
-        nc.vector.tensor_copy(
-            out=rows_by_t[:].rearrange("p t (b r) -> p t b r", r=RUN),
-            in_=rows[:].rearrange("p (b t r) -> p t b r", t=PACK, r=RUN),
-        )
-        gb_ps = psum_mm.tile([P, PACK, P], BF16, name="gb_ps", tag="acc")
-        for t in range(PACK):
-            nc.tensor.transpose(gb_ps[:, t, :], rows_by_t[:, t, :], ident_bf[:])
-        g_col = keep.tile([P, PACK], F32, name="g_col")
-        nc.vector.tensor_copy(out=g_col[:], in_=gb_ps[:, :, 2])
-        b_col = keep.tile([P, PACK], F32, name="b_col")
-        nc.vector.tensor_copy(out=b_col[:], in_=gb_ps[:, :, 3])
 
-        for step in range(-1, UNITS + 3):
+        for step in range(0, UNITS + 3):
             if step % 2 == 0:
                 load_attn((step + 6) // 2)
                 load_x((step + 4) // 2)
-            add_bl(step - 2, 0)
             add_bl(step - 2, 1)
-            add_bo2(step + 2)
             add_first_product(step + 1)
-            add_second_product(step - 3)
+            if step < UNITS:
+                add_second_product(step - 3)
             normalise(step - 1)
             z_transpose(step - 1)
             squares(step, 0)
@@ -387,10 +394,27 @@ def tile_successiveswintransfomerblock_pb_t_kernel(tc, attn_win, x_mid, Wo2, bo2
             gain_and_bias(step - 1)
             regroup_h(step - 2, nc.vector)
             quantise_attn(step + 2)
-            norm_shift(step)
             product(step + 2, "a", wo_codes, wo_scales)
+            add_bl(step - 1, 0)
+            add_bo2(step + 3)
+            norm_shift(step)
             if step == 0:
-                wl_codes, wl_scales = quantise_weight(nc, stage, keep, wl_raw, "wl")
+                rows_by_t = keep.tile([P, PACK, P], BF16, name="rows_by_t")
+                nc.vector.tensor_copy(
+                    out=rows_by_t[:].rearrange("p t (b r) -> p t b r", r=RUN),
+                    in_=rows[:].rearrange("p (b t r) -> p t b r", t=PACK, r=RUN),
+                )
+                gb_ps = psum_mm.tile([P, PACK, P], BF16, name="gb_ps", tag="acc")
+                for t in range(PACK):
+                    nc.tensor.transpose(gb_ps[:, t, :], rows_by_t[:, t, :], ident_bf[:])
+                g_col = keep.tile([P, PACK], F32, name="g_col")
+                nc.vector.tensor_copy(out=g_col[:], in_=gb_ps[:, :, 2])
+                b_col = keep.tile([P, PACK], F32, name="b_col")
+                nc.vector.tensor_copy(out=b_col[:], in_=gb_ps[:, :, 3])
+            if step == 1:
+                wl_codes, wl_scales = quantise_weight(nc, keep, regroup_weight(nc, stage, wl_raw, "wl"), "wl")
             quantise_h(step - 2)
-            if step > 0:
+            if step > 1:
                 product(step - 2, "h", wl_codes, wl_scales)
+            if step >= UNITS:
+                add_second_product(step - 3)

@@ -30,7 +30,7 @@ ROW_QUADS = 16
 SHIFT_TOKENS = GROUP // 2
 LN_EPS = 1e-5
 EARLY = 2
-SCALAR_TOKENS = 96
+SCALAR_TOKENS = 176
 
 FLOPS = 2 * 2 * IMAGES * IMAGE_TOKENS * D * D
 
@@ -191,7 +191,7 @@ def tile_successiveswintransfomerblock_pb_t_kernel(tc, attn_win, x_mid, Wo2, bo2
             for s in range(SLOTS):
                 early = u < EARLY
                 engine = nc.vector if early else nc.gpsimd
-                x = resid.tile([P, D], F32, name="x", tag="x%d" % s, bufs=4 + s)
+                x = resid.tile([P, D], F32, name="x", tag="x%d" % s, bufs=6)
                 engine.tensor_tensor(
                     out=x[:],
                     in0=bo2_ps[:] if early else bo2_all[:],
@@ -254,19 +254,19 @@ def tile_successiveswintransfomerblock_pb_t_kernel(tc, attn_win, x_mid, Wo2, bo2
             )
             live["shift", u] = shift
 
-        def normalise(u):
+        def normalise(u, engine, s):
             if not 0 <= u < UNITS:
                 return
-            z = work.tile([P, SLOTS, D], F32, name="z")
-            for s in range(SLOTS):
-                nc.scalar.activation(
-                    out=z[:, s, :].rearrange("p (t b r) -> p t b r", t=PACK, r=RUN),
-                    in_=live["x", u, s][:].rearrange("p (b t r) -> p t b r", t=PACK, r=RUN),
-                    func=ACT.Identity,
-                    bias=live["shift", u][:, s : s + 1],
-                    scale=live["rstd", u][:, s : s + 1],
-                )
-            live["z", u] = z
+            if engine == nc.gpsimd:
+                live["z", u] = work.tile([P, SLOTS, D], F32, name="z")
+            z_by_t = live["z", u][:, s, :].rearrange("p (t b r) -> p t b r", t=PACK, r=RUN)
+            x_by_t = live["x", u, s][:].rearrange("p (b t r) -> p t b r", t=PACK, r=RUN)
+            rstd = live["rstd", u][:, s : s + 1]
+            shift = live["shift", u][:, s : s + 1]
+            if engine == nc.gpsimd:
+                nc.gpsimd.tensor_scalar(out=z_by_t, in0=x_by_t, scalar1=rstd, scalar2=shift, op0=MULT, op1=ADD)
+            else:
+                nc.scalar.activation(out=z_by_t, in_=x_by_t, func=ACT.Identity, bias=shift, scale=rstd)
 
         def z_transpose(u):
             if not 0 <= u < UNITS:
@@ -379,11 +379,12 @@ def tile_successiveswintransfomerblock_pb_t_kernel(tc, attn_win, x_mid, Wo2, bo2
             if step % 2 == 0:
                 load_attn((step + 6) // 2)
                 load_x((step + 4) // 2)
+            add_bl(step - 2, 0)
             add_bl(step - 2, 1)
             add_first_product(step + 1)
             if step < UNITS:
                 add_second_product(step - 3)
-            normalise(step - 1)
+            normalise(step - 1, nc.scalar, 0)
             z_transpose(step - 1)
             squares(step, 0)
             squares(step, 1)
@@ -395,9 +396,9 @@ def tile_successiveswintransfomerblock_pb_t_kernel(tc, attn_win, x_mid, Wo2, bo2
             regroup_h(step - 2, nc.vector)
             quantise_attn(step + 2)
             product(step + 2, "a", wo_codes, wo_scales)
-            add_bl(step - 1, 0)
-            add_bo2(step + 3)
             norm_shift(step)
+            normalise(step, nc.gpsimd, 1)
+            add_bo2(step + 3)
             if step == 0:
                 rows_by_t = keep.tile([P, PACK, P], BF16, name="rows_by_t")
                 nc.vector.tensor_copy(

@@ -112,12 +112,12 @@ def tile_successiveswintransfomerblock_pb_t_kernel(tc, attn_win, x_mid, Wo2, bo2
         nc.sync.dma_start(out=wo_raw[:], in_=Wo2.rearrange("(p t) n -> p t n", t=PACK))
         for r, vec in enumerate((bo2, bl, g4, b4)):
             nc.sync.dma_start(out=rows[r : r + 1, :], in_=vec.rearrange("(o d) -> o d", o=1))
-        load_attn(0, 1)
-        load_x(0)
-        load_attn(1)
         wl_raw = stage.tile([P, PACK, D], BF16, name="wl_raw")
         for t in range(PACK):
             nc.sync.dma_start(out=wl_raw[:, t, :], in_=Wl.rearrange("(b t r) n -> t b r n", t=PACK, r=RUN)[t])
+        load_attn(0, 1)
+        load_x(0)
+        load_attn(1)
 
         ident = keep.tile([P, P], F32, name="ident")
         make_identity(nc, ident[:])
@@ -188,17 +188,17 @@ def tile_successiveswintransfomerblock_pb_t_kernel(tc, attn_win, x_mid, Wo2, bo2
         def add_bo2(u):
             if not 0 <= u < UNITS:
                 return
+            x = resid.tile([P, SLOTS, D], F32, name="x", bufs=6)
+            engine = nc.vector if u < EARLY else nc.gpsimd
+            bias = bo2_ps if u < EARLY else bo2_all
+            engine.tensor_tensor(
+                out=x[:],
+                in0=bias[:].unsqueeze(1).to_broadcast([P, SLOTS, D]),
+                in1=live["xm_sb", u // 2][:, slots(u), :],
+                op=ADD,
+            )
             for s in range(SLOTS):
-                early = u < EARLY
-                engine = nc.vector if early else nc.gpsimd
-                x = resid.tile([P, D], F32, name="x", tag="x%d" % s, bufs=6)
-                engine.tensor_tensor(
-                    out=x[:],
-                    in0=bo2_ps[:] if early else bo2_all[:],
-                    in1=live["xm_sb", u // 2][:, u % 2 * SLOTS + s, :],
-                    op=ADD,
-                )
-                live["x", u, s] = x
+                live["x", u, s] = x[:, s, :]
 
         def add_first_product(u):
             if not 0 <= u < UNITS:
@@ -207,10 +207,10 @@ def tile_successiveswintransfomerblock_pb_t_kernel(tc, attn_win, x_mid, Wo2, bo2
             for s in range(SLOTS):
                 x = live["x", u, s]
                 nc.vector.scalar_tensor_tensor(
-                    out=x[:],
+                    out=x,
                     in0=live["a_acc", u, s][:],
                     scalar=1.0,
-                    in1=x[:],
+                    in1=x,
                     op0=MULT,
                     op1=ADD,
                     accum_out=x_sum[:, s : s + 1],
@@ -225,7 +225,7 @@ def tile_successiveswintransfomerblock_pb_t_kernel(tc, attn_win, x_mid, Wo2, bo2
             junk = work.tile([P, D], BF16, name="junk")
             nc.scalar.activation(
                 out=junk[:],
-                in_=live["x", u, s][:],
+                in_=live["x", u, s],
                 func=ACT.Square,
                 bias=live["x_sum", u][:, s : s + 1],
                 scale=-float(D),
@@ -260,7 +260,7 @@ def tile_successiveswintransfomerblock_pb_t_kernel(tc, attn_win, x_mid, Wo2, bo2
             if engine == nc.gpsimd:
                 live["z", u] = work.tile([P, SLOTS, D], F32, name="z")
             z_by_t = live["z", u][:, s, :].rearrange("p (t b r) -> p t b r", t=PACK, r=RUN)
-            x_by_t = live["x", u, s][:].rearrange("p (b t r) -> p t b r", t=PACK, r=RUN)
+            x_by_t = live["x", u, s].rearrange("p (b t r) -> p t b r", t=PACK, r=RUN)
             rstd = live["rstd", u][:, s : s + 1]
             shift = live["shift", u][:, s : s + 1]
             if engine == nc.gpsimd:
@@ -326,7 +326,7 @@ def tile_successiveswintransfomerblock_pb_t_kernel(tc, attn_win, x_mid, Wo2, bo2
                 return
             if s == 0:
                 live["y", u] = resid.tile([P, SLOTS, D], F32, name="y")
-            nc.vector.tensor_tensor(out=live["y", u][:, s, :], in0=bl_all[:], in1=live["x", u, s][:], op=ADD)
+            nc.vector.tensor_tensor(out=live["y", u][:, s, :], in0=bl_all[:], in1=live["x", u, s], op=ADD)
 
         def add_second_product(u):
             if not 0 <= u < UNITS:
@@ -355,6 +355,7 @@ def tile_successiveswintransfomerblock_pb_t_kernel(tc, attn_win, x_mid, Wo2, bo2
         attn_transpose(0)
         attn_copy_out(0)
         wo_grouped = regroup_weight(nc, stage, wo_raw, "wo")
+        wl_grouped = regroup_weight(nc, stage, wl_raw, "wl")
         quantise_attn(0)
         wo_codes, wo_scales = quantise_weight(nc, keep, wo_grouped, "wo")
         attn_transpose(1)
@@ -413,7 +414,7 @@ def tile_successiveswintransfomerblock_pb_t_kernel(tc, attn_win, x_mid, Wo2, bo2
                 b_col = keep.tile([P, PACK], F32, name="b_col")
                 nc.vector.tensor_copy(out=b_col[:], in_=gb_ps[:, :, 3])
             if step == 1:
-                wl_codes, wl_scales = quantise_weight(nc, keep, regroup_weight(nc, stage, wl_raw, "wl"), "wl")
+                wl_codes, wl_scales = quantise_weight(nc, keep, wl_grouped, "wl")
             quantise_h(step - 2)
             if step > 1:
                 product(step - 2, "h", wl_codes, wl_scales)

@@ -30,7 +30,7 @@ ROW_QUADS = 16
 SHIFT_TOKENS = GROUP // 2
 LN_EPS = 1e-5
 EARLY = 2
-SCALAR_TOKENS = 176
+SCALAR_TOKENS = 208
 
 FLOPS = 2 * 2 * IMAGES * IMAGE_TOKENS * D * D
 
@@ -197,15 +197,14 @@ def tile_successiveswintransfomerblock_pb_t_kernel(tc, attn_win, x_mid, Wo2, bo2
                 in1=live["xm_sb", u // 2][:, slots(u), :],
                 op=ADD,
             )
-            for s in range(SLOTS):
-                live["x", u, s] = x[:, s, :]
+            live["x", u] = x
 
         def add_first_product(u):
             if not 0 <= u < UNITS:
                 return
             x_sum = stats.tile([P, SLOTS], F32, name="x_sum")
             for s in range(SLOTS):
-                x = live["x", u, s]
+                x = live["x", u][:, s, :]
                 nc.vector.scalar_tensor_tensor(
                     out=x,
                     in0=live["a_acc", u, s][:],
@@ -225,7 +224,7 @@ def tile_successiveswintransfomerblock_pb_t_kernel(tc, attn_win, x_mid, Wo2, bo2
             junk = work.tile([P, D], BF16, name="junk")
             nc.scalar.activation(
                 out=junk[:],
-                in_=live["x", u, s],
+                in_=live["x", u][:, s, :],
                 func=ACT.Square,
                 bias=live["x_sum", u][:, s : s + 1],
                 scale=-float(D),
@@ -260,7 +259,7 @@ def tile_successiveswintransfomerblock_pb_t_kernel(tc, attn_win, x_mid, Wo2, bo2
             if engine == nc.gpsimd:
                 live["z", u] = work.tile([P, SLOTS, D], F32, name="z")
             z_by_t = live["z", u][:, s, :].rearrange("p (t b r) -> p t b r", t=PACK, r=RUN)
-            x_by_t = live["x", u, s].rearrange("p (b t r) -> p t b r", t=PACK, r=RUN)
+            x_by_t = live["x", u][:, s, :].rearrange("p (b t r) -> p t b r", t=PACK, r=RUN)
             rstd = live["rstd", u][:, s : s + 1]
             shift = live["shift", u][:, s : s + 1]
             if engine == nc.gpsimd:
@@ -321,12 +320,14 @@ def tile_successiveswintransfomerblock_pb_t_kernel(tc, attn_win, x_mid, Wo2, bo2
             live["h_codes", u] = h_codes
             live["h_scales", u] = h_scales
 
-        def add_bl(u, s):
+        def add_bl(u):
             if not 0 <= u < UNITS:
                 return
-            if s == 0:
-                live["y", u] = resid.tile([P, SLOTS, D], F32, name="y")
-            nc.vector.tensor_tensor(out=live["y", u][:, s, :], in0=bl_all[:], in1=live["x", u, s], op=ADD)
+            y = resid.tile([P, SLOTS, D], F32, name="y")
+            nc.vector.tensor_tensor(
+                out=y[:], in0=bl_all[:].unsqueeze(1).to_broadcast([P, SLOTS, D]), in1=live["x", u][:], op=ADD
+            )
+            live["y", u] = y
 
         def add_second_product(u):
             if not 0 <= u < UNITS:
@@ -380,8 +381,7 @@ def tile_successiveswintransfomerblock_pb_t_kernel(tc, attn_win, x_mid, Wo2, bo2
             if step % 2 == 0:
                 load_attn((step + 6) // 2)
                 load_x((step + 4) // 2)
-            add_bl(step - 2, 0)
-            add_bl(step - 2, 1)
+            add_bl(step - 2)
             add_first_product(step + 1)
             if step < UNITS:
                 add_second_product(step - 3)

@@ -30,7 +30,7 @@ ROW_QUADS = 16
 SHIFT_TOKENS = GROUP // 2
 LN_EPS = 1e-5
 EARLY = 2
-SCALAR_TOKENS = 208
+SCALAR_TOKENS = 192
 
 FLOPS = 2 * 2 * IMAGES * IMAGE_TOKENS * D * D
 
@@ -389,10 +389,10 @@ def tile_successiveswintransfomerblock_pb_t_kernel(tc, attn_win, x_mid, Wo2, bo2
             z_transpose(step - 1)
             squares(step, 0)
             squares(step, 1)
+            regroup_h(step - 2, nc.scalar)
+            inverse_deviation(step)
             attn_copy_out(step + 3)
             attn_transpose(step + 4)
-            inverse_deviation(step)
-            regroup_h(step - 2, nc.scalar)
             gain_and_bias(step - 1)
             regroup_h(step - 2, nc.vector)
             quantise_attn(step + 2)

from contextlib import ExitStack

import concourse.mybir as mybir
from concourse.masks import make_identity

F32 = mybir.dt.float32
BF16 = mybir.dt.bfloat16
U32 = mybir.dt.uint32
U8 = mybir.dt.uint8
FP8X4 = mybir.dt.float8_e4m3fn_x4
ADD = mybir.AluOpType.add
MULT = mybir.AluOpType.mult
ACT = mybir.ActivationFunctionType

P = 128
D = 512
PACK = 4
RUN = 8
QUAD = 4
GROUP = P * QUAD
SLOTS = 2
UNIT = P * SLOTS
IMAGES = 2
WINDOW_ROWS = 8
WS = 8
GROUPS = IMAGES * WINDOW_ROWS
UNITS = GROUPS * QUAD // SLOTS
IMAGE_TOKENS = WINDOW_ROWS * GROUP
ROW_QUADS = 16
SHIFT_TOKENS = GROUP // 2
LN_EPS = 1e-5
EARLY = 2
SCALAR_TOKENS = 192

FLOPS = 2 * 2 * IMAGES * IMAGE_TOKENS * D * D


def quads(flat, first, count):
    return flat[first : first + count, :].rearrange("(p q) d -> p q d", q=QUAD)


def image_pieces(g):
    image, window_row = divmod(g, WINDOW_ROWS)
    base = image * IMAGE_TOKENS
    if window_row == 0:
        half = P // 2
        return [(0, half, base + IMAGE_TOKENS - SHIFT_TOKENS), (half, half, base)]
    return [(0, P, base + window_row * GROUP - SHIFT_TOKENS)]


def regroup_weight(nc, stage, raw, label):
    grouped = stage.tile([P, D, PACK], BF16, name="grouped_" + label, align_bytes=64)
    nc.vector.tensor_copy(out=grouped[:], in_=raw[:].rearrange("p t n -> p n t"))
    return grouped


def quantise_weight(nc, keep, grouped, label):
    codes = keep.tile([P, D], U32, name="codes_" + label, align_bytes=64)
    scales = keep.tile([P, D], U8, name="scales_" + label, align_bytes=64)
    nc.vector.quantize_mx(
        out=codes[:].bitcast(FP8X4), scales=scales[:], in_=grouped[:].rearrange("p n t -> p (n t)")
    )
    return codes, scales


def tile_successiveswintransfomerblock_pb_t_kernel(tc, attn_win, x_mid, Wo2, bo2, g4, b4, Wl, bl, out):
    nc = tc.nc
    attn_flat = attn_win.flatten_outer_dims()
    x_flat = x_mid.flatten_outer_dims()
    out_flat = out.flatten_outer_dims()

    with ExitStack() as ctx:
        keep = ctx.enter_context(tc.tile_pool(name="keep", bufs=1))
        stage = ctx.enter_context(tc.tile_pool(name="stage", bufs=1))
        loads = ctx.enter_context(tc.tile_pool(name="loads", bufs=4))
        work = ctx.enter_context(tc.tile_pool(name="work", bufs=3))
        resid = ctx.enter_context(tc.tile_pool(name="resid", bufs=4))
        stats = ctx.enter_context(tc.tile_pool(name="stats", bufs=4))
        psum_keep = ctx.enter_context(tc.psum_pool(name="psum_keep", bufs=1))
        psum_at = ctx.enter_context(tc.psum_pool(name="psum_at", bufs=1))
        psum_mm = ctx.enter_context(tc.psum_pool(name="psum_mm", bufs=4))
        psum_zt = ctx.enter_context(tc.psum_pool(name="psum_zt", bufs=2))
        ctx.enter_context(tc.manual_schedule())

        live = {}

        def load_attn(g, half=None):
            if not 0 <= g < GROUPS:
                return
            if half != 1:
                live["attn_sb", g] = loads.tile([P, QUAD, D], BF16, name="attn_sb")
            part = slice(0, QUAD) if half is None else slice(half * SLOTS, half * SLOTS + SLOTS)
            nc.sync.dma_start(out=live["attn_sb", g][:, part, :], in_=quads(attn_flat, g * GROUP, GROUP)[:, part, :])

        def load_x(g):
            if not 0 <= g < GROUPS:
                return
            xm_sb = loads.tile([P, QUAD, D], BF16, name="xm_sb")
            for first_p, n_p, first_token in image_pieces(g):
                nc.sync.dma_start(out=xm_sb[first_p : first_p + n_p], in_=quads(x_flat, first_token, n_p * QUAD))
            live["xm_sb", g] = xm_sb

        eps_col = keep.tile([P, 1], F32, name="eps_col")
        nc.vector.memset(eps_col[:], LN_EPS)
        table_warm = keep.tile([P, 1], F32, name="table_warm")
        nc.scalar.activation(out=table_warm[:], in_=eps_col[:], func=ACT.Abs_reciprocal_sqrt)
        rows = keep.tile([P, D], BF16, name="rows")
        nc.vector.memset(rows[:], 0.0)

        load_attn(0, 0)
        wo_raw = stage.tile([P, PACK, D], BF16, name="wo_raw")
        nc.sync.dma_start(out=wo_raw[:], in_=Wo2.rearrange("(p t) n -> p t n", t=PACK))
        for r, vec in enumerate((bo2, bl, g4, b4)):
            nc.sync.dma_start(out=rows[r : r + 1, :], in_=vec.rearrange("(o d) -> o d", o=1))
        wl_raw = stage.tile([P, PACK, D], BF16, name="wl_raw")
        for t in range(PACK):
            nc.sync.dma_start(out=wl_raw[:, t, :], in_=Wl.rearrange("(b t r) n -> t b r n", t=PACK, r=RUN)[t])
        load_attn(0, 1)
        load_x(0)
        load_attn(1)

        ident = keep.tile([P, P], F32, name="ident")
        make_identity(nc, ident[:])
        by_row = keep.tile([P, P], F32, name="by_row")
        nc.vector.tensor_copy(
            out=by_row[:].rearrange("p (r w h) -> p r w h", r=WS, w=WS),
            in_=ident[:].rearrange("p (w r h) -> p r w h", w=WS, r=WS),
        )
        to_image = keep.tile([P, P], F32, name="to_image")
        unrolled = by_row[:].rearrange("p (r m) -> p r m", m=ROW_QUADS)
        rolled = to_image[:].rearrange("p (r m) -> p r m", m=ROW_QUADS)
        nc.vector.tensor_copy(out=rolled[:, :, 0 : ROW_QUADS - 1], in_=unrolled[:, :, 1:ROW_QUADS])
        nc.vector.tensor_copy(out=rolled[:, :, ROW_QUADS - 1 : ROW_QUADS], in_=unrolled[:, :, 0:1])
        ident_bf = keep.tile([P, P], BF16, name="ident_bf")
        nc.vector.tensor_copy(out=ident_bf[:], in_=ident[:])


        def slots(u):
            return slice(u % 2 * SLOTS, u % 2 * SLOTS + SLOTS)

        def attn_transpose(u):
            if not 0 <= u < UNITS:
                return
            attn_words = live["attn_sb", u // 2][:, slots(u), :].bitcast(F32)
            a_t = psum_at.tile([P, SLOTS, 2, P], F32, name="a_t")
            for s in range(SLOTS):
                for v in range(2):
                    nc.tensor.transpose(a_t[:, s, v, :], attn_words[:, s, v : 2 * P : 2], to_image[:])
            live["a_t", u] = a_t

        def attn_copy_out(u):
            if not 0 <= u < UNITS:
                return
            a_grouped = work.tile([P, SLOTS, P, PACK], BF16, name="a_grouped", align_bytes=64)
            nc.scalar.copy(out=a_grouped[:].bitcast(F32), in_=live["a_t", u][:].rearrange("p s v r -> p s r v"))
            live["a_grouped", u] = a_grouped

        def quantise_attn(u):
            if not 0 <= u < UNITS:
                return
            a_codes = work.tile([P, UNIT], U32, name="a_codes", align_bytes=64)
            a_scales = work.tile([P, UNIT], U8, name="a_scales", align_bytes=64)
            nc.vector.quantize_mx(
                out=a_codes[:].bitcast(FP8X4),
                scales=a_scales[:],
                in_=live["a_grouped", u][:].rearrange("p s r t -> p (s r t)"),
            )
            live["a_codes", u] = a_codes
            live["a_scales", u] = a_scales

        def product(u, label, codes, scales):
            if not 0 <= u < UNITS:
                return
            for s in range(SLOTS):
                tokens = slice(s * P, (s + 1) * P)
                acc = psum_mm.tile([P, D], F32, name="acc")
                nc.tensor.matmul_mx(
                    out=acc[:],
                    lhsT=live[label + "_codes", u][:, tokens].bitcast(FP8X4),
                    lhsT_scale=live[label + "_scales", u][:, tokens],
                    rhs=codes[:].bitcast(FP8X4),
                    rhs_scale=scales[:],
                    start=True,
                    stop=True,
                )
                live[label + "_acc", u, s] = acc

        def add_bo2(u):
            if not 0 <= u < UNITS:
                return
            x = resid.tile([P, SLOTS, D], F32, name="x", bufs=6)
            engine = nc.vector if u < EARLY else nc.gpsimd
            bias = bo2_ps if u < EARLY else bo2_all
            engine.tensor_tensor(
                out=x[:],
                in0=bias[:].unsqueeze(1).to_broadcast([P, SLOTS, D]),
                in1=live["xm_sb", u // 2][:, slots(u), :],
                op=ADD,
            )
            live["x", u] = x

        def add_first_product(u):
            if not 0 <= u < UNITS:
                return
            x_sum = stats.tile([P, SLOTS], F32, name="x_sum")
            for s in range(SLOTS):
                x = live["x", u][:, s, :]
                nc.vector.scalar_tensor_tensor(
                    out=x,
                    in0=live["a_acc", u, s][:],
                    scalar=1.0,
                    in1=x,
                    op0=MULT,
                    op1=ADD,
                    accum_out=x_sum[:, s : s + 1],
                )
            live["x_sum", u] = x_sum

        def squares(u, s):
            if not 0 <= u < UNITS:
                return
            if s == 0:
                live["sq_sum", u] = stats.tile([P, SLOTS], F32, name="sq_sum")
            junk = work.tile([P, D], BF16, name="junk")
            nc.scalar.activation(
                out=junk[:],
                in_=live["x", u][:, s, :],
                func=ACT.Square,
                bias=live["x_sum", u][:, s : s + 1],
                scale=-float(D),
                accum_out=live["sq_sum", u][:, s : s + 1],
            )

        def inverse_deviation(u):
            if not 0 <= u < UNITS:
                return
            rstd = stats.tile([P, SLOTS], F32, name="rstd")
            nc.scalar.activation(
                out=rstd[:],
                in_=live["sq_sum", u][:],
                func=ACT.Abs_reciprocal_sqrt,
                bias=eps_col[:],
                scale=1.0 / (D * D * D),
            )
            live["rstd", u] = rstd

        def norm_shift(u):
            if not 0 <= u < UNITS:
                return
            shift = stats.tile([P, SLOTS], F32, name="shift")
            nc.vector.scalar_tensor_tensor(
                out=shift[:], in0=live["x_sum", u][:], scalar=-1.0 / D, in1=live["rstd", u][:], op0=MULT, op1=MULT
            )
            live["shift", u] = shift

        def normalise(u, engine, s):
            if not 0 <= u < UNITS:
                return
            if engine == nc.gpsimd:
                live["z", u] = work.tile([P, SLOTS, D], F32, name="z")
            z_by_t = live["z", u][:, s, :].rearrange("p (t b r) -> p t b r", t=PACK, r=RUN)
            x_by_t = live["x", u][:, s, :].rearrange("p (b t r) -> p t b r", t=PACK, r=RUN)
            rstd = live["rstd", u][:, s : s + 1]
            shift = live["shift", u][:, s : s + 1]
            if engine == nc.gpsimd:
                nc.gpsimd.tensor_scalar(out=z_by_t, in0=x_by_t, scalar1=rstd, scalar2=shift, op0=MULT, op1=ADD)
            else:
                nc.scalar.activation(out=z_by_t, in_=x_by_t, func=ACT.Identity, bias=shift, scale=rstd)

        def z_transpose(u):
            if not 0 <= u < UNITS:
                return
            banks = []
            for half in range(2):
                z_t = psum_zt.tile([P, 2, UNIT], F32, name="z_t")
                banks.append(z_t)
            for s in range(SLOTS):
                for t in range(PACK):
                    nc.tensor.transpose(
                        banks[t // 2][:, t % 2, s * P : (s + 1) * P], live["z", u][:, s, t * P : (t + 1) * P], ident[:]
                    )
            live["z_t", u] = banks

        def gain_and_bias(u):
            if not 0 <= u < UNITS:
                return
            h_t = work.tile([P, PACK, UNIT], BF16, name="h_t")
            for t in range(PACK):
                nc.scalar.activation(
                    out=h_t[:, t, :],
                    in_=live["z_t", u][t // 2][:, t % 2, :],
                    func=ACT.Identity,
                    bias=b_col[:, t : t + 1],
                    scale=g_col[:, t : t + 1],
                )
            live["h_t", u] = h_t

        def regroup_h(u, engine):
            if not 0 <= u < UNITS:
                return
            if engine == nc.scalar:
                live["h_grouped", u] = work.tile([P, UNIT, PACK], BF16, name="h_grouped", align_bytes=64)
            tokens = slice(0, SCALAR_TOKENS) if engine == nc.scalar else slice(SCALAR_TOKENS, UNIT)
            copy = nc.scalar.copy if engine == nc.scalar else nc.vector.tensor_copy
            copy(
                out=live["h_grouped", u][:, tokens, :].rearrange("p (c i) t -> p c t i", i=4),
                in_=live["h_t", u][:, :, tokens].rearrange("p t (c i) -> p c t i", i=4),
            )

        def quantise_h(u):
            if not 0 <= u < UNITS:
                return
            h_codes = work.tile([P, UNIT], U32, name="h_codes", align_bytes=64)
            h_scales = work.tile([P, UNIT], U8, name="h_scales", align_bytes=64)
            nc.vector.quantize_mx(
                out=h_codes[:].bitcast(FP8X4),
                scales=h_scales[:],
                in_=live["h_grouped", u][:].rearrange("p r t -> p (r t)"),
            )
            live["h_codes", u] = h_codes
            live["h_scales", u] = h_scales

        def add_bl(u):
            if not 0 <= u < UNITS:
                return
            y = resid.tile([P, SLOTS, D], F32, name="y")
            nc.vector.tensor_tensor(
                out=y[:], in0=bl_all[:].unsqueeze(1).to_broadcast([P, SLOTS, D]), in1=live["x", u][:], op=ADD
            )
            live["y", u] = y

        def add_second_product(u):
            if not 0 <= u < UNITS:
                return
            y = live["y", u]
            pieces = SLOTS if u == UNITS - 1 else 1
            for s in range(SLOTS):
                nc.vector.tensor_tensor(out=y[:, s, :], in0=live["h_acc", u, s][:], in1=y[:, s, :], op=ADD)
                if (s + 1) % (SLOTS // pieces) == 0:
                    done = slice(s + 1 - SLOTS // pieces, s + 1)
                    in_quad = slice(slots(u).start + done.start, slots(u).start + done.stop)
                    for first_p, n_p, first_token in image_pieces(u // 2):
                        nc.sync.dma_start(
                            out=quads(out_flat, first_token, n_p * QUAD)[:, in_quad, :],
                            in_=y[first_p : first_p + n_p, done, :],
                        )

        def spread(target, r):
            nc.tensor.matmul(
                target[:], lhsT=ident_bf[:, r : r + 1].to_broadcast([P, P]), rhs=rows[:], start=True, stop=True
            )

        bo2_ps = psum_mm.tile([P, D], F32, name="bo2_ps", tag="acc")
        spread(bo2_ps, 0)
        bo2_all = keep.tile([P, D], BF16, name="bo2_all")
        attn_transpose(0)
        attn_copy_out(0)
        wo_grouped = regroup_weight(nc, stage, wo_raw, "wo")
        wl_grouped = regroup_weight(nc, stage, wl_raw, "wl")
        quantise_attn(0)
        wo_codes, wo_scales = quantise_weight(nc, keep, wo_grouped, "wo")
        attn_transpose(1)
        attn_copy_out(1)
        product(0, "a", wo_codes, wo_scales)
        add_bo2(0)
        quantise_attn(1)
        attn_transpose(2)
        nc.scalar.copy(out=bo2_all[:], in_=bo2_ps[:])
        attn_copy_out(2)
        product(1, "a", wo_codes, wo_scales)
        add_first_product(0)
        add_bo2(1)
        load_x(1)
        load_attn(2)
        add_bo2(2)
        attn_transpose(3)
        bl_all = psum_keep.tile([P, D], F32, name="bl_all")
        spread(bl_all, 1)

        for step in range(0, UNITS + 3):
            if step % 2 == 0:
                load_attn((step + 6) // 2)
                load_x((step + 4) // 2)
            add_bl(step - 2)
            add_first_product(step + 1)
            if step < UNITS:
                add_second_product(step - 3)
            normalise(step - 1, nc.scalar, 0)
            z_transpose(step - 1)
            squares(step, 0)
            squares(step, 1)
            regroup_h(step - 2, nc.scalar)
            inverse_deviation(step)
            attn_copy_out(step + 3)
            attn_transpose(step + 4)
            gain_and_bias(step - 1)
            regroup_h(step - 2, nc.vector)
            quantise_attn(step + 2)
            product(step + 2, "a", wo_codes, wo_scales)
            norm_shift(step)
            normalise(step, nc.gpsimd, 1)
            add_bo2(step + 3)
            if step == 0:
                rows_by_t = keep.tile([P, PACK, P], BF16, name="rows_by_t")
                nc.vector.tensor_copy(
                    out=rows_by_t[:].rearrange("p t (b r) -> p t b r", r=RUN),
                    in_=rows[:].rearrange("p (b t r) -> p t b r", t=PACK, r=RUN),
                )
                gb_ps = psum_mm.tile([P, PACK, P], BF16, name="gb_ps", tag="acc")
                for t in range(PACK):
                    nc.tensor.transpose(gb_ps[:, t, :], rows_by_t[:, t, :], ident_bf[:])
                g_col = keep.tile([P, PACK], F32, name="g_col")
                nc.vector.tensor_copy(out=g_col[:], in_=gb_ps[:, :, 2])
                b_col = keep.tile([P, PACK], F32, name="b_col")
                nc.vector.tensor_copy(out=b_col[:], in_=gb_ps[:, :, 3])
            if step == 1:
                wl_codes, wl_scales = quantise_weight(nc, keep, wl_grouped, "wl")
            quantise_h(step - 2)
            if step > 1:
                product(step - 2, "h", wl_codes, wl_scales)
            if step >= UNITS:
                add_second_product(step - 3)
